import numpy as np
import ml_dtypes


def mxq(x, axis, fmt="e4m3"):
    dtype, down = {"e4m3": (ml_dtypes.float8_e4m3fn, 7), "e5m2": (ml_dtypes.float8_e5m2, 14)}[fmt]
    v = np.moveaxis(np.asarray(x, np.float32).astype(ml_dtypes.bfloat16).astype(np.float64), axis, -1)
    blocks = v.reshape(v.shape[:-1] + (-1, 32))
    amax = np.abs(blocks).max(-1, keepdims=True)
    byte = np.maximum(np.where(amax > 0, np.frexp(amax)[1] - 1 + 127, 0) - down, 1)
    scale = np.exp2(byte - 127.0)
    codes = (blocks / scale).astype(np.float32).astype(dtype).astype(np.float64)
    return np.moveaxis((codes * scale).reshape(v.shape), -1, axis)


WIDE = False


def mx_kscale(k):
    if not WIDE:
        return np.ones(k)
    levels = np.array([10, -10, 5, -5, 0])
    a = np.random.permutation(np.resize(levels, k // 512 * 4)).reshape(k // 512, 4)
    idx = np.arange(k)
    return np.exp2(a[idx // 512, idx % 128 // 32])


BF16 = ml_dtypes.bfloat16


def bf(x):
    return np.asarray(x, np.float32).astype(BF16)


def f64(x):
    return np.asarray(x).astype(np.float64)


E2M1 = np.array([0.0, 0.5, 1.0, 1.5, 2.0, 3.0, 4.0, 6.0, -0.0, -0.5, -1.0, -1.5, -2.0, -3.0, -4.0, -6.0])


def pack_weight(w, fmt):
    k, n = w.shape
    w = f64(bf(w)).reshape(k // 32, 32, n)
    amax = np.abs(w).max(1)
    if fmt == "e4m3":
        byte = np.frexp(amax)[1] - 1 + 127 - 7
    else:
        mant, ex = np.frexp(amax / 6.0)
        byte = np.where(mant > 0.5, ex, ex - 1) + 127
    byte = np.clip(np.where(amax > 0, byte, 1), 1, 254)
    scaled = (w * np.exp2(127.0 - byte)[:, None, :]).reshape(k, n).astype(np.float32)
    by_word = np.ascontiguousarray(scaled.reshape(k // 512, 128, 4, n).transpose(0, 1, 3, 2))
    if fmt == "e4m3":
        words = by_word.astype(ml_dtypes.float8_e4m3fn).view(np.uint8)
    else:
        c = by_word.astype(ml_dtypes.float4_e2m1fn).view(np.uint8) & 0xF
        words = c[..., 0::2] | (c[..., 1::2] << 4)
    return np.ascontiguousarray(words), np.ascontiguousarray(byte.astype(np.uint8).reshape(k // 512, 16, n))


def unpack_weight(words, scales, fmt):
    g, p, n, _ = words.shape
    if fmt == "e4m3":
        vals = np.ascontiguousarray(words).view(ml_dtypes.float8_e4m3fn).astype(np.float64)
    else:
        nib = np.empty((g, p, n, 4), np.uint8)
        nib[..., 0::2] = words & 0xF
        nib[..., 1::2] = words >> 4
        vals = E2M1[nib]
    vals = vals * np.repeat(np.exp2(scales.astype(np.float64) - 127.0), 8, axis=1)[..., None]
    return vals.transpose(0, 1, 3, 2).reshape(g * 512, n)


B, N, D_IN, H, D_HEAD, D_EXPAND = 4, 256, 512, 16, 128, 512
D_V = D_IN * H
EPS = 1e-5


def feature_norm(x, gamma, beta):
    mean = x.mean(axis=1, keepdims=True)
    var = x.var(axis=1, keepdims=True)
    return gamma * (x - mean) / np.sqrt(var + EPS) + beta


def setup_inputs():
    t = mx_kscale(D_V)
    s = mx_kscale(D_IN)
    attn_out = bf(5.0 * np.random.standard_normal((B, N, D_V)) * t)
    x = bf(1.5 * np.random.standard_normal((B, N, D_IN)))
    W_merge_words, W_merge_scales = pack_weight(np.random.standard_normal((D_V, D_IN)) * 0.2 / np.sqrt(D_V) / t[:, None], "e4m3")
    b_merge = bf(0.3 * np.random.standard_normal(D_IN))
    gamma2 = bf((1.0 + 0.1 * np.random.standard_normal((1, 1, D_IN))) * s)
    beta2 = bf(0.2 * np.random.standard_normal((1, 1, D_IN)) * s)
    W1_words, W1_scales = pack_weight(np.random.standard_normal((D_IN, D_EXPAND)) / np.sqrt(D_IN) / s[:, None], "e4m3")
    b1 = bf(0.2 * np.random.standard_normal(D_EXPAND))
    return {"attn_out": attn_out,
            "x": x,
            "W_merge_words": W_merge_words,
            "W_merge_scales": W_merge_scales,
            "b_merge": b_merge,
            "gamma2": gamma2,
            "beta2": beta2,
            "W1_words": W1_words,
            "W1_scales": W1_scales,
            "b1": b1}


def reference(attn_out, x, W_merge_words, W_merge_scales, b_merge, gamma2, beta2, W1_words, W1_scales, b1):
    x2 = f64(x) + (mxq(f64(attn_out), 2, "e4m3") @ unpack_weight(W_merge_words, W_merge_scales, "e4m3")) + f64(b_merge)
    xn = feature_norm(x2, f64(gamma2), f64(beta2))
    ffh = (mxq(xn, 2, "e4m3") @ unpack_weight(W1_words, W1_scales, "e4m3")) + f64(b1)
    return x2, ffh

@@ -1,0 +1,288 @@
+from contextlib import ExitStack
+
+import concourse.mybir as mybir
+from concourse.masks import make_identity
+
+FP8X4 = mybir.dt.float8_e4m3fn_x4
+BF16 = mybir.dt.bfloat16
+F32 = mybir.dt.float32
+I32 = mybir.dt.int32
+U32 = mybir.dt.uint32
+U8 = mybir.dt.uint8
+ALU = mybir.AluOpType
+ACT = mybir.ActivationFunctionType
+
+P = 128
+PACK = 4
+K_PASS = P * PACK
+HALVES = 2
+
+BATCH = 4
+TOKENS = 256
+TILES = TOKENS // P
+D_V = 8192
+D = 512
+EPS = 1e-5
+
+GROUPS = D_V // K_PASS
+ROUND_GROUPS = 4
+ROUND_K = ROUND_GROUPS * K_PASS
+ROUNDS_PER_BATCH = GROUPS // ROUND_GROUPS
+ROUNDS = BATCH * ROUNDS_PER_BATCH
+ATTN_BUFS = 12
+
+FLOPS = 2 * BATCH * TOKENS * D_V * D + 2 * BATCH * TOKENS * D * D
+
+
+def batch_ending_at(round_index):
+    if 0 <= round_index < ROUNDS and round_index % ROUNDS_PER_BATCH == ROUNDS_PER_BATCH - 1:
+        return round_index // ROUNDS_PER_BATCH
+    return None
+
+
+def tile_attentionblock_pc_k_kernel(
+    tc, attn_out, x, W_merge_words, W_merge_scales, b_merge, gamma2, beta2, W1_words, W1_scales, b1, out_0, out_1
+):
+    nc = tc.nc
+    with ExitStack() as ctx:
+        ctx.enter_context(tc.manual_schedule())
+        const = ctx.enter_context(tc.tile_pool(name="const", bufs=1))
+        attn_pool = ctx.enter_context(tc.tile_pool(name="attn", bufs=ATTN_BUFS))
+        x_pool = ctx.enter_context(tc.tile_pool(name="x", bufs=BATCH))
+        stage = ctx.enter_context(tc.tile_pool(name="stage", bufs=2))
+        tail = ctx.enter_context(tc.tile_pool(name="tail", bufs=2))
+        acc_pool = ctx.enter_context(tc.psum_pool(name="acc", bufs=1))
+        work = ctx.enter_context(tc.psum_pool(name="work", bufs=6))
+
+        bias_rows = const.tile([P, 2, D], BF16)
+        nc.vector.memset(bias_rows[:], 0.0)
+        nc.scalar.dma_start(out=bias_rows[0:1, 0, :], in_=b_merge.unsqueeze(0))
+        nc.scalar.dma_start(out=bias_rows[0:1, 1, :], in_=b1.unsqueeze(0))
+        gamma = const.tile([P, PACK], BF16)
+        beta = const.tile([P, PACK], BF16)
+        nc.scalar.dma_start(out=gamma[:], in_=gamma2.rearrange("a b (p t) -> (a b p) t", t=PACK))
+        nc.scalar.dma_start(out=beta[:], in_=beta2.rearrange("a b (p t) -> (a b p) t", t=PACK))
+        ones = const.tile([P, P], BF16)
+        nc.vector.memset(ones[:], 1.0)
+        eps = const.tile([P, 1], F32)
+        nc.vector.memset(eps[:], EPS)
+        w_planes = const.tile([P, GROUPS + 1, D], U8, align_bytes=64)
+        nc.vector.memset(w_planes[:].bitcast(I32), 0)
+        ident = const.tile([P, P], F32)
+        make_identity(nc, ident[:])
+        table_warm = const.tile([P, 1], F32)
+        nc.scalar.activation(out=table_warm[:], in_=eps[:], func=ACT.Sqrt)
+
+        w_words = const.tile([P, GROUPS, D], U32, align_bytes=64)
+        w1_words = const.tile([P, D], U32, align_bytes=64)
+
+        attn_rows = attn_out.rearrange("b (p i) k -> b p i k", i=TILES)
+        attn_of = {}
+        x_of = {}
+
+        def load_attn(r):
+            b, part = divmod(r, ROUNDS_PER_BATCH)
+            attn_tile = attn_pool.tile([P, TILES, ROUND_K], BF16)
+            nc.sync.dma_start(out=attn_tile[:], in_=attn_rows[b, :, :, part * ROUND_K : (part + 1) * ROUND_K])
+            attn_of[r] = attn_tile
+            if batch_ending_at(r) is not None:
+                x_tile = x_pool.tile([P, TILES, D], BF16)
+                nc.sync.dma_start(out=x_tile[:], in_=x[b].rearrange("(p i) f -> p i f", i=TILES))
+                x_of[b] = x_tile
+
+        def load_scale_planes():
+            rows = W_merge_scales.rearrange("g q n -> q g n")
+            for low in range(2 * PACK):
+                quadrant, row = divmod(low, PACK)
+                nc.sync.dma_start(
+                    out=w_planes[32 * quadrant + row : P : 64, 0:GROUPS, :].bitcast(I32),
+                    in_=rows[low : 4 * PACK : 2 * PACK].bitcast(I32),
+                )
+            for row in range(PACK):
+                nc.sync.dma_start(
+                    out=w_planes[row:P:32, GROUPS, :].bitcast(I32),
+                    in_=W1_scales[0, row : 4 * PACK : PACK, :].bitcast(I32),
+                )
+
+        def load_merge_weights(part):
+            groups = slice(part * ROUND_GROUPS, (part + 1) * ROUND_GROUPS)
+            nc.sync.dma_start(
+                out=w_words[:, groups, :].bitcast(I32),
+                in_=W_merge_words[groups].rearrange("g p n t -> p g (n t)").bitcast(I32),
+            )
+
+        load_attn(0)
+        load_scale_planes()
+        for part in range(ROUNDS_PER_BATCH):
+            load_merge_weights(part)
+            load_attn(part + 1)
+        nc.sync.dma_start(out=w1_words[:].bitcast(I32), in_=W1_words[0].rearrange("p n t -> p (n t)").bitcast(I32))
+        for r in range(ROUNDS_PER_BATCH + 1, ATTN_BUFS):
+            load_attn(r)
+
+        bias_all = const.tile([P, 2, D], F32)
+        for j in range(2):
+            spread = work.tile([P, D], F32, tag="work")
+            nc.tensor.matmul(out=spread[:], lhsT=ones[:], rhs=bias_rows[:, j, :], start=True, stop=True)
+            nc.vector.tensor_copy(out=bias_all[:, j, :], in_=spread[:])
+
+        banks_of = {}
+        codes_of = {}
+        acc_of = {}
+
+        def transpose_round(r):
+            words = attn_of[r][:].bitcast(F32)
+            pairs = K_PASS // 2
+            banks_of[r] = []
+            for g in range(ROUND_GROUPS):
+                bank = work.tile([P, HALVES, TOKENS], F32, tag="work")
+                for i in range(TILES):
+                    for u in range(HALVES):
+                        nc.tensor.transpose(
+                            bank[:, u, i * P : (i + 1) * P], words[:, i, g * pairs + u : (g + 1) * pairs : HALVES], ident[:]
+                        )
+                banks_of[r].append(bank)
+
+        def quantise_round(r):
+            grouped = stage.tile([P, ROUND_GROUPS, TOKENS * PACK], BF16, align_bytes=64)
+            grouped_words = grouped[:].bitcast(F32)
+            for g in range(ROUND_GROUPS):
+                nc.scalar.copy(
+                    out=grouped_words[:, g, :].rearrange("p (k u) -> p k u", u=HALVES),
+                    in_=banks_of[r][g][:].rearrange("p u k -> p k u"),
+                )
+            codes = stage.tile([P, ROUND_GROUPS * TOKENS], U32, align_bytes=64)
+            scales = stage.tile([P, ROUND_GROUPS * TOKENS], U8, align_bytes=64)
+            nc.vector.quantize_mx(
+                out=codes[:].bitcast(FP8X4), scales=scales[:], in_=grouped[:].rearrange("p g c -> p (g c)")
+            )
+            codes_of[r] = (codes, scales)
+
+        def merge_passes(r):
+            b, part = divmod(r, ROUNDS_PER_BATCH)
+            if part == 0:
+                acc_of[b] = [acc_pool.tile([P, D], F32, name="acc%d" % i) for i in range(TILES)]
+            codes, scales = codes_of[r]
+            for g in range(ROUND_GROUPS):
+                group = part * ROUND_GROUPS + g
+                for i in range(TILES):
+                    cols = slice(g * TOKENS + i * P, g * TOKENS + (i + 1) * P)
+                    nc.tensor.matmul_mx(
+                        out=acc_of[b][i][:],
+                        lhsT=codes[:, cols].bitcast(FP8X4),
+                        lhsT_scale=scales[:, cols],
+                        rhs=w_words[:, group, :].bitcast(FP8X4),
+                        rhs_scale=w_planes[:, group, :],
+                        start=(group == 0),
+                        stop=(group == GROUPS - 1),
+                    )
+
+        xb_of = {}
+        x2_of = {}
+        x2T_of = {}
+        xn_of = {}
+
+        def prepare_residual(b):
+            xb = tail.tile([P, TILES, D], F32)
+            nc.vector.tensor_tensor(
+                out=xb[:], in0=x_of[b][:], in1=bias_all[:, 0, :].unsqueeze(1).to_broadcast([P, TILES, D]), op=ALU.add
+            )
+            xb_of[b] = xb
+
+        def residual(b):
+            x2 = tail.tile([P, TILES, D], F32)
+            for i in range(TILES):
+                nc.vector.tensor_tensor(out=x2[:, i, :], in0=acc_of[b][i][:], in1=xb_of[b][:, i, :], op=ALU.add)
+            nc.sync.dma_start(out=out_0[b].rearrange("(p i) f -> p i f", i=TILES), in_=x2[:])
+            x2_of[b] = x2
+
+        def transpose_x2(b):
+            x2T_of[b] = [work.tile([P, 2, TOKENS], F32, tag="work", name="x2T%d" % h) for h in range(2)]
+            for t in range(PACK):
+                for i in range(TILES):
+                    nc.tensor.transpose(
+                        x2T_of[b][t // 2][:, t % 2, i * P : (i + 1) * P], x2_of[b][:, i, t:D:PACK], ident[:]
+                    )
+
+        def normalise(b):
+            columns = [x2T_of[b][t // 2][:, t % 2, :] for t in range(PACK)]
+            stats = tail.tile([P, PACK, 6], F32)
+            mean_var = tail.tile([P, PACK, 2], F32)
+            for t in range(PACK):
+                nc.vector.bn_stats(out=stats[:, t, :], in_=columns[t])
+            for t in range(PACK):
+                nc.vector.bn_aggr(out=mean_var[:, t, :], in_=stats[:, t, :])
+            std = tail.tile([P, PACK], F32)
+            nc.scalar.activation(out=std[:], in_=mean_var[:, :, 1], func=ACT.Sqrt, bias=eps[:, 0:1], scale=1.0)
+            gain = tail.tile([P, PACK], F32)
+            shift = tail.tile([P, PACK], F32)
+            nc.vector.reciprocal(out=gain[:], in_=std[:])
+            nc.vector.tensor_tensor(out=gain[:], in0=gain[:], in1=gamma[:], op=ALU.mult)
+            nc.vector.tensor_tensor(out=shift[:], in0=mean_var[:, :, 0], in1=gain[:], op=ALU.mult)
+            nc.vector.tensor_tensor(out=shift[:], in0=beta[:], in1=shift[:], op=ALU.subtract)
+            xnT = tail.tile([P, PACK, TOKENS], BF16)
+            for t in range(PACK):
+                if t < PACK // 2:
+                    nc.scalar.activation(
+                        out=xnT[:, t, :], in_=columns[t], func=ACT.Identity, bias=shift[:, t : t + 1], scale=gain[:, t : t + 1]
+                    )
+                else:
+                    nc.vector.tensor_scalar(
+                        out=xnT[:, t, :],
+                        in0=columns[t],
+                        scalar1=gain[:, t : t + 1],
+                        scalar2=shift[:, t : t + 1],
+                        op0=ALU.mult,
+                        op1=ALU.add,
+                    )
+            xn_grouped = tail.tile([P, TOKENS, PACK], BF16, align_bytes=64)
+            nc.vector.tensor_copy(out=xn_grouped[:], in_=xnT[:].rearrange("p t k -> p k t"))
+            xn_codes = tail.tile([P, TOKENS], U32, align_bytes=64)
+            xn_scales = tail.tile([P, TOKENS], U8, align_bytes=64)
+            nc.vector.quantize_mx(
+                out=xn_codes[:].bitcast(FP8X4), scales=xn_scales[:], in_=xn_grouped[:].rearrange("p k t -> p (k t)")
+            )
+            xn_of[b] = (xn_codes, xn_scales)
+
+        def expand(b):
+            xn_codes, xn_scales = xn_of[b]
+            products = [work.tile([P, D], F32, tag="work", name="ffh_ps%d" % i) for i in range(TILES)]
+            for i in range(TILES):
+                cols = slice(i * P, (i + 1) * P)
+                nc.tensor.matmul_mx(
+                    out=products[i][:],
+                    lhsT=xn_codes[:, cols].bitcast(FP8X4),
+                    lhsT_scale=xn_scales[:, cols],
+                    rhs=w1_words[:].bitcast(FP8X4),
+                    rhs_scale=w_planes[:, GROUPS, :],
+                    start=True,
+                    stop=True,
+                )
+            ffh = tail.tile([P, TILES, D], F32)
+            for i in range(TILES):
+                nc.vector.tensor_tensor(out=ffh[:, i, :], in0=products[i][:], in1=bias_all[:, 1, :], op=ALU.add)
+            nc.sync.dma_start(out=out_1[b].rearrange("(p i) f -> p i f", i=TILES), in_=ffh[:])
+
+        for step in range(ROUNDS + 3):
+            ended_now = batch_ending_at(step)
+            ended_1 = batch_ending_at(step - 1)
+            ended_2 = batch_ending_at(step - 2)
+            ended_3 = batch_ending_at(step - 3)
+            if step < ROUNDS:
+                transpose_round(step)
+            if ended_2 is not None:
+                transpose_x2(ended_2)
+            if step < ROUNDS:
+                quantise_round(step)
+            if ended_2 is not None:
+                normalise(ended_2)
+            if 1 <= step <= ROUNDS:
+                merge_passes(step - 1)
+            if ended_3 is not None:
+                expand(ended_3)
+            if ended_1 is not None:
+                residual(ended_1)
+            if ended_now is not None:
+                prepare_residual(ended_now)
+            if step + ATTN_BUFS < ROUNDS:
+                load_attn(step + ATTN_BUFS)

@@ -80,15 +80,21 @@ def tile_attentionblock_pc_k_kernel(
         attn_of = {}
         x_of = {}
 
-        def load_attn(r):
+        def load_attn(r, pieces):
             b, part = divmod(r, ROUNDS_PER_BATCH)
             attn_tile = attn_pool.tile([P, TILES, ROUND_K], BF16)
-            nc.sync.dma_start(out=attn_tile[:], in_=attn_rows[b, :, :, part * ROUND_K : (part + 1) * ROUND_K])
+            width = ROUND_K // pieces
+            for piece in range(pieces):
+                nc.sync.dma_start(
+                    out=attn_tile[:, :, piece * width : (piece + 1) * width],
+                    in_=attn_rows[b, :, :, part * ROUND_K + piece * width : part * ROUND_K + (piece + 1) * width],
+                )
             attn_of[r] = attn_tile
-            if batch_ending_at(r) is not None:
-                x_tile = x_pool.tile([P, TILES, D], BF16)
-                nc.sync.dma_start(out=x_tile[:], in_=x[b].rearrange("(p i) f -> p i f", i=TILES))
-                x_of[b] = x_tile
+
+        def load_x(b):
+            x_tile = x_pool.tile([P, TILES, D], BF16)
+            nc.sync.dma_start(out=x_tile[:], in_=x[b].rearrange("(p i) f -> p i f", i=TILES))
+            x_of[b] = x_tile
 
         def load_scale_planes():
             rows = W_merge_scales.rearrange("g q n -> q g n")
@@ -98,11 +104,6 @@ def tile_attentionblock_pc_k_kernel(
                     out=w_planes[32 * quadrant + row : P : 64, 0:GROUPS, :].bitcast(I32),
                     in_=rows[low : 4 * PACK : 2 * PACK].bitcast(I32),
                 )
-            for row in range(PACK):
-                nc.sync.dma_start(
-                    out=w_planes[row:P:32, GROUPS, :].bitcast(I32),
-                    in_=W1_scales[0, row : 4 * PACK : PACK, :].bitcast(I32),
-                )
 
         def load_merge_weights(part):
             groups = slice(part * ROUND_GROUPS, (part + 1) * ROUND_GROUPS)
@@ -111,14 +112,28 @@ def tile_attentionblock_pc_k_kernel(
                 in_=W_merge_words[groups].rearrange("g p n t -> p g (n t)").bitcast(I32),
             )
 
-        load_attn(0)
-        load_scale_planes()
-        for part in range(ROUNDS_PER_BATCH):
-            load_merge_weights(part)
-            load_attn(part + 1)
-        nc.sync.dma_start(out=w1_words[:].bitcast(I32), in_=W1_words[0].rearrange("p n t -> p (n t)").bitcast(I32))
-        for r in range(ROUNDS_PER_BATCH + 1, ATTN_BUFS):
-            load_attn(r)
+        def load_expand_weights():
+            nc.sync.dma_start(out=w1_words[:].bitcast(I32), in_=W1_words[0].rearrange("p n t -> p (n t)").bitcast(I32))
+            for row in range(PACK):
+                nc.sync.dma_start(
+                    out=w_planes[row:P:32, GROUPS, :].bitcast(I32),
+                    in_=W1_scales[0, row : 4 * PACK : PACK, :].bitcast(I32),
+                )
+
+        def load_for_step(step):
+            if step < ROUNDS:
+                load_attn(step, ROUND_GROUPS if step == 0 else 1)
+            if step == 1:
+                load_scale_planes()
+            if 1 <= step <= ROUNDS_PER_BATCH:
+                load_merge_weights(step - 1)
+            if batch_ending_at(step - 1) is not None:
+                load_x(batch_ending_at(step - 1))
+            if step == ROUNDS_PER_BATCH:
+                load_expand_weights()
+
+        for step in range(ATTN_BUFS):
+            load_for_step(step)
 
         bias_all = const.tile([P, 2, D], F32)
         for j in range(2):
@@ -198,8 +213,8 @@ def tile_attentionblock_pc_k_kernel(
 
         def transpose_x2(b):
             x2T_of[b] = [work.tile([P, 2, TOKENS], F32, tag="work", name="x2T%d" % h) for h in range(2)]
-            for t in range(PACK):
-                for i in range(TILES):
+            for i in range(TILES):
+                for t in range(PACK):
                     nc.tensor.transpose(
                         x2T_of[b][t // 2][:, t % 2, i * P : (i + 1) * P], x2_of[b][:, i, t:D:PACK], ident[:]
                     )
@@ -259,12 +274,12 @@ def tile_attentionblock_pc_k_kernel(
                     stop=True,
                 )
             ffh = tail.tile([P, TILES, D], F32)
+            ffh_rows = out_1[b].rearrange("(p i) f -> p i f", i=TILES)
             for i in range(TILES):
                 nc.vector.tensor_tensor(out=ffh[:, i, :], in0=products[i][:], in1=bias_all[:, 1, :], op=ALU.add)
-            nc.sync.dma_start(out=out_1[b].rearrange("(p i) f -> p i f", i=TILES), in_=ffh[:])
+                nc.sync.dma_start(out=ffh_rows[:, i, :], in_=ffh[:, i, :])
 
         for step in range(ROUNDS + 3):
-            ended_now = batch_ending_at(step)
             ended_1 = batch_ending_at(step - 1)
             ended_2 = batch_ending_at(step - 2)
             ended_3 = batch_ending_at(step - 3)
@@ -272,6 +287,8 @@ def tile_attentionblock_pc_k_kernel(
                 transpose_round(step)
             if ended_2 is not None:
                 transpose_x2(ended_2)
+            if ended_1 is not None:
+                prepare_residual(ended_1)
             if step < ROUNDS:
                 quantise_round(step)
             if ended_2 is not None:
@@ -282,7 +299,5 @@ def tile_attentionblock_pc_k_kernel(
                 expand(ended_3)
             if ended_1 is not None:
                 residual(ended_1)
-            if ended_now is not None:
-                prepare_residual(ended_now)
-            if step + ATTN_BUFS < ROUNDS:
-                load_attn(step + ATTN_BUFS)
+            if step + ATTN_BUFS <= ROUNDS:
+                load_for_step(step + ATTN_BUFS)

@@ -66,8 +66,10 @@ def tile_attentionblock_pc_k_kernel(
         nc.vector.memset(ones[:], 1.0)
         eps = const.tile([P, 1], F32)
         nc.vector.memset(eps[:], EPS)
-        w_planes = const.tile([P, GROUPS + 1, D], U8, align_bytes=64)
+        w_planes = const.tile([P, GROUPS, D], U8, align_bytes=64)
         nc.vector.memset(w_planes[:].bitcast(I32), 0)
+        w1_plane = const.tile([P, D], U8, align_bytes=64)
+        nc.vector.memset(w1_plane[:].bitcast(I32), 0)
         ident = const.tile([P, P], F32)
         make_identity(nc, ident[:])
         table_warm = const.tile([P, 1], F32)
@@ -101,7 +103,7 @@ def tile_attentionblock_pc_k_kernel(
             for low in range(2 * PACK):
                 quadrant, row = divmod(low, PACK)
                 nc.sync.dma_start(
-                    out=w_planes[32 * quadrant + row : P : 64, 0:GROUPS, :].bitcast(I32),
+                    out=w_planes[32 * quadrant + row : P : 64, :, :].bitcast(I32),
                     in_=rows[low : 4 * PACK : 2 * PACK].bitcast(I32),
                 )
 
@@ -116,7 +118,7 @@ def tile_attentionblock_pc_k_kernel(
             nc.sync.dma_start(out=w1_words[:].bitcast(I32), in_=W1_words[0].rearrange("p n t -> p (n t)").bitcast(I32))
             for row in range(PACK):
                 nc.sync.dma_start(
-                    out=w_planes[row:P:32, GROUPS, :].bitcast(I32),
+                    out=w1_plane[row:P:32, :].bitcast(I32),
                     in_=W1_scales[0, row : 4 * PACK : PACK, :].bitcast(I32),
                 )
 
@@ -136,10 +138,12 @@ def tile_attentionblock_pc_k_kernel(
             load_for_step(step)
 
         bias_all = const.tile([P, 2, D], F32)
-        for j in range(2):
-            spread = work.tile([P, D], F32, tag="work")
-            nc.tensor.matmul(out=spread[:], lhsT=ones[:], rhs=bias_rows[:, j, :], start=True, stop=True)
-            nc.vector.tensor_copy(out=bias_all[:, j, :], in_=spread[:])
+
+        def spread_biases():
+            for j in range(2):
+                spread = work.tile([P, D], F32, tag="work")
+                nc.tensor.matmul(out=spread[:], lhsT=ones[:], rhs=bias_rows[:, j, :], start=True, stop=True)
+                nc.vector.tensor_copy(out=bias_all[:, j, :], in_=spread[:])
 
         banks_of = {}
         codes_of = {}
@@ -269,7 +273,7 @@ def tile_attentionblock_pc_k_kernel(
                     lhsT=xn_codes[:, cols].bitcast(FP8X4),
                     lhsT_scale=xn_scales[:, cols],
                     rhs=w1_words[:].bitcast(FP8X4),
-                    rhs_scale=w_planes[:, GROUPS, :],
+                    rhs_scale=w1_plane[:],
                     start=True,
                     stop=True,
                 )
@@ -293,6 +297,8 @@ def tile_attentionblock_pc_k_kernel(
                 quantise_round(step)
             if ended_2 is not None:
                 normalise(ended_2)
+            if step == 0:
+                spread_biases()
             if 1 <= step <= ROUNDS:
                 merge_passes(step - 1)
             if ended_3 is not None:

@@ -26,10 +26,11 @@ EPS = 1e-5
 
 GROUPS = D_V // K_PASS
 ROUND_GROUPS = 4
+BANK_GROUPS = 2
 ROUND_K = ROUND_GROUPS * K_PASS
 ROUNDS_PER_BATCH = GROUPS // ROUND_GROUPS
 ROUNDS = BATCH * ROUNDS_PER_BATCH
-ATTN_BUFS = 12
+ATTN_BUFS = 10
 
 FLOPS = 2 * BATCH * TOKENS * D_V * D + 2 * BATCH * TOKENS * D * D
 
@@ -82,15 +83,15 @@ def tile_attentionblock_pc_k_kernel(
         attn_of = {}
         x_of = {}
 
-        def load_attn(r, pieces):
+        def load_attn(r, by_token_tile):
             b, part = divmod(r, ROUNDS_PER_BATCH)
+            columns = slice(part * ROUND_K, (part + 1) * ROUND_K)
             attn_tile = attn_pool.tile([P, TILES, ROUND_K], BF16)
-            width = ROUND_K // pieces
-            for piece in range(pieces):
-                nc.sync.dma_start(
-                    out=attn_tile[:, :, piece * width : (piece + 1) * width],
-                    in_=attn_rows[b, :, :, part * ROUND_K + piece * width : part * ROUND_K + (piece + 1) * width],
-                )
+            if by_token_tile:
+                for i in range(TILES):
+                    nc.sync.dma_start(out=attn_tile[:, i, :], in_=attn_rows[b, :, i, columns])
+            else:
+                nc.sync.dma_start(out=attn_tile[:], in_=attn_rows[b, :, :, columns])
             attn_of[r] = attn_tile
 
         def load_x(b):
@@ -124,7 +125,7 @@ def tile_attentionblock_pc_k_kernel(
 
         def load_for_step(step):
             if step < ROUNDS:
-                load_attn(step, ROUND_GROUPS if step == 0 else 1)
+                load_attn(step, by_token_tile=(step == 0))
             if step == 1:
                 load_scale_planes()
             if 1 <= step <= ROUNDS_PER_BATCH:
@@ -145,36 +146,45 @@ def tile_attentionblock_pc_k_kernel(
                 nc.tensor.matmul(out=spread[:], lhsT=ones[:], rhs=bias_rows[:, j, :], start=True, stop=True)
                 nc.vector.tensor_copy(out=bias_all[:, j, :], in_=spread[:])
 
+        sorted_of = {}
         banks_of = {}
         codes_of = {}
         acc_of = {}
 
-        def transpose_round(r):
+        def sort_round(r):
             words = attn_of[r][:].bitcast(F32)
-            pairs = K_PASS // 2
-            banks_of[r] = []
-            for g in range(ROUND_GROUPS):
-                bank = work.tile([P, HALVES, TOKENS], F32, tag="work")
-                for i in range(TILES):
-                    for u in range(HALVES):
-                        nc.tensor.transpose(
-                            bank[:, u, i * P : (i + 1) * P], words[:, i, g * pairs + u : (g + 1) * pairs : HALVES], ident[:]
-                        )
-                banks_of[r].append(bank)
+            sorted_words = stage.tile([P, TILES, ROUND_GROUPS, HALVES, P], F32)
+            for i in range(TILES):
+                nc.vector.tensor_copy(
+                    out=sorted_words[:, i], in_=words[:, i, :].rearrange("p (g j u) -> p g u j", g=ROUND_GROUPS, u=HALVES)
+                )
+            sorted_of[r] = sorted_words
+            if r + ATTN_BUFS <= ROUNDS:
+                load_for_step(r + ATTN_BUFS)
+
+        def transpose_round(r):
+            for i in range(TILES):
+                for first in range(0, ROUND_GROUPS, BANK_GROUPS):
+                    bank = work.tile([P, BANK_GROUPS, HALVES, P], F32, tag="work")
+                    for g in range(BANK_GROUPS):
+                        for u in range(HALVES):
+                            nc.tensor.transpose(bank[:, g, u, :], sorted_of[r][:, i, first + g, u, :], ident[:])
+                    banks_of[(r, i, first)] = bank
 
         def quantise_round(r):
-            grouped = stage.tile([P, ROUND_GROUPS, TOKENS * PACK], BF16, align_bytes=64)
+            grouped = stage.tile([P, TILES, ROUND_GROUPS, P * PACK], BF16, align_bytes=64)
             grouped_words = grouped[:].bitcast(F32)
-            for g in range(ROUND_GROUPS):
-                nc.scalar.copy(
-                    out=grouped_words[:, g, :].rearrange("p (k u) -> p k u", u=HALVES),
-                    in_=banks_of[r][g][:].rearrange("p u k -> p k u"),
+            codes = stage.tile([P, TILES, ROUND_GROUPS * P], U32, align_bytes=64)
+            scales = stage.tile([P, TILES, ROUND_GROUPS * P], U8, align_bytes=64)
+            for i in range(TILES):
+                for first in range(0, ROUND_GROUPS, BANK_GROUPS):
+                    nc.scalar.copy(
+                        out=grouped_words[:, i, first : first + BANK_GROUPS, :].rearrange("p g (k u) -> p g k u", u=HALVES),
+                        in_=banks_of[(r, i, first)][:].rearrange("p g u k -> p g k u"),
+                    )
+                nc.vector.quantize_mx(
+                    out=codes[:, i, :].bitcast(FP8X4), scales=scales[:, i, :], in_=grouped[:, i].rearrange("p g c -> p (g c)")
                 )
-            codes = stage.tile([P, ROUND_GROUPS * TOKENS], U32, align_bytes=64)
-            scales = stage.tile([P, ROUND_GROUPS * TOKENS], U8, align_bytes=64)
-            nc.vector.quantize_mx(
-                out=codes[:].bitcast(FP8X4), scales=scales[:], in_=grouped[:].rearrange("p g c -> p (g c)")
-            )
             codes_of[r] = (codes, scales)
 
         def merge_passes(r):
@@ -182,14 +192,14 @@ def tile_attentionblock_pc_k_kernel(
             if part == 0:
                 acc_of[b] = [acc_pool.tile([P, D], F32, name="acc%d" % i) for i in range(TILES)]
             codes, scales = codes_of[r]
-            for g in range(ROUND_GROUPS):
-                group = part * ROUND_GROUPS + g
-                for i in range(TILES):
-                    cols = slice(g * TOKENS + i * P, g * TOKENS + (i + 1) * P)
+            for i in range(TILES):
+                for g in range(ROUND_GROUPS):
+                    group = part * ROUND_GROUPS + g
+                    cols = slice(g * P, (g + 1) * P)
                     nc.tensor.matmul_mx(
                         out=acc_of[b][i][:],
-                        lhsT=codes[:, cols].bitcast(FP8X4),
-                        lhsT_scale=scales[:, cols],
+                        lhsT=codes[:, i, cols].bitcast(FP8X4),
+                        lhsT_scale=scales[:, i, cols],
                         rhs=w_words[:, group, :].bitcast(FP8X4),
                         rhs_scale=w_planes[:, group, :],
                         start=(group == 0),
@@ -283,6 +293,7 @@ def tile_attentionblock_pc_k_kernel(
                 nc.vector.tensor_tensor(out=ffh[:, i, :], in0=products[i][:], in1=bias_all[:, 1, :], op=ALU.add)
                 nc.sync.dma_start(out=ffh_rows[:, i, :], in_=ffh[:, i, :])
 
+        sort_round(0)
         for step in range(ROUNDS + 3):
             ended_1 = batch_ending_at(step - 1)
             ended_2 = batch_ending_at(step - 2)
@@ -293,6 +304,8 @@ def tile_attentionblock_pc_k_kernel(
                 transpose_x2(ended_2)
             if ended_1 is not None:
                 prepare_residual(ended_1)
+            if step + 1 < ROUNDS:
+                sort_round(step + 1)
             if step < ROUNDS:
                 quantise_round(step)
             if ended_2 is not None:
@@ -305,5 +318,3 @@ def tile_attentionblock_pc_k_kernel(
                 expand(ended_3)
             if ended_1 is not None:
                 residual(ended_1)
-            if step + ATTN_BUFS <= ROUNDS:
-                load_for_step(step + ATTN_BUFS)

@@ -151,16 +151,12 @@ def tile_attentionblock_pc_k_kernel(
         codes_of = {}
         acc_of = {}
 
-        def sort_round(r):
+        def open_sorted(r):
+            sorted_of[r] = stage.tile([P, TILES, ROUND_GROUPS, HALVES, P], F32, name="sorted_words")
+
+        def sort_tile(r, i, copy):
             words = attn_of[r][:].bitcast(F32)
-            sorted_words = stage.tile([P, TILES, ROUND_GROUPS, HALVES, P], F32)
-            for i in range(TILES):
-                nc.vector.tensor_copy(
-                    out=sorted_words[:, i], in_=words[:, i, :].rearrange("p (g j u) -> p g u j", g=ROUND_GROUPS, u=HALVES)
-                )
-            sorted_of[r] = sorted_words
-            if r + ATTN_BUFS <= ROUNDS:
-                load_for_step(r + ATTN_BUFS)
+            copy(out=sorted_of[r][:, i], in_=words[:, i, :].rearrange("p (g j u) -> p g u j", g=ROUND_GROUPS, u=HALVES))
 
         def transpose_round(r):
             for i in range(TILES):
@@ -187,24 +183,23 @@ def tile_attentionblock_pc_k_kernel(
                 )
             codes_of[r] = (codes, scales)
 
-        def merge_passes(r):
+        def merge_passes(r, i):
             b, part = divmod(r, ROUNDS_PER_BATCH)
             if part == 0:
-                acc_of[b] = [acc_pool.tile([P, D], F32, name="acc%d" % i) for i in range(TILES)]
+                acc_of[(b, i)] = acc_pool.tile([P, D], F32, name="acc%d" % i)
             codes, scales = codes_of[r]
-            for i in range(TILES):
-                for g in range(ROUND_GROUPS):
-                    group = part * ROUND_GROUPS + g
-                    cols = slice(g * P, (g + 1) * P)
-                    nc.tensor.matmul_mx(
-                        out=acc_of[b][i][:],
-                        lhsT=codes[:, i, cols].bitcast(FP8X4),
-                        lhsT_scale=scales[:, i, cols],
-                        rhs=w_words[:, group, :].bitcast(FP8X4),
-                        rhs_scale=w_planes[:, group, :],
-                        start=(group == 0),
-                        stop=(group == GROUPS - 1),
-                    )
+            for g in range(ROUND_GROUPS):
+                group = part * ROUND_GROUPS + g
+                cols = slice(g * P, (g + 1) * P)
+                nc.tensor.matmul_mx(
+                    out=acc_of[(b, i)][:],
+                    lhsT=codes[:, i, cols].bitcast(FP8X4),
+                    lhsT_scale=scales[:, i, cols],
+                    rhs=w_words[:, group, :].bitcast(FP8X4),
+                    rhs_scale=w_planes[:, group, :],
+                    start=(group == 0),
+                    stop=(group == GROUPS - 1),
+                )
 
         xb_of = {}
         x2_of = {}
@@ -221,7 +216,7 @@ def tile_attentionblock_pc_k_kernel(
         def residual(b):
             x2 = tail.tile([P, TILES, D], F32)
             for i in range(TILES):
-                nc.vector.tensor_tensor(out=x2[:, i, :], in0=acc_of[b][i][:], in1=xb_of[b][:, i, :], op=ALU.add)
+                nc.vector.tensor_tensor(out=x2[:, i, :], in0=acc_of[(b, i)][:], in1=xb_of[b][:, i, :], op=ALU.add)
             nc.sync.dma_start(out=out_0[b].rearrange("(p i) f -> p i f", i=TILES), in_=x2[:])
             x2_of[b] = x2
 
@@ -293,27 +288,36 @@ def tile_attentionblock_pc_k_kernel(
                 nc.vector.tensor_tensor(out=ffh[:, i, :], in0=products[i][:], in1=bias_all[:, 1, :], op=ALU.add)
                 nc.sync.dma_start(out=ffh_rows[:, i, :], in_=ffh[:, i, :])
 
-        sort_round(0)
+        open_sorted(0)
+        sort_tile(0, 0, nc.vector.tensor_copy)
+        sort_tile(0, 1, nc.scalar.copy)
+        load_for_step(ATTN_BUFS)
         for step in range(ROUNDS + 3):
             ended_1 = batch_ending_at(step - 1)
             ended_2 = batch_ending_at(step - 2)
             ended_3 = batch_ending_at(step - 3)
             if step < ROUNDS:
                 transpose_round(step)
-            if ended_2 is not None:
-                transpose_x2(ended_2)
             if ended_1 is not None:
                 prepare_residual(ended_1)
             if step + 1 < ROUNDS:
-                sort_round(step + 1)
+                open_sorted(step + 1)
+                sort_tile(step + 1, 0, nc.vector.tensor_copy)
             if step < ROUNDS:
                 quantise_round(step)
-            if ended_2 is not None:
-                normalise(ended_2)
+            if step + 1 < ROUNDS:
+                sort_tile(step + 1, 1, nc.scalar.copy)
+            if step + 1 + ATTN_BUFS <= ROUNDS:
+                load_for_step(step + 1 + ATTN_BUFS)
             if step == 0:
                 spread_biases()
             if 1 <= step <= ROUNDS:
-                merge_passes(step - 1)
+                merge_passes(step - 1, 0)
+            if ended_2 is not None:
+                transpose_x2(ended_2)
+                normalise(ended_2)
+            if 1 <= step <= ROUNDS:
+                merge_passes(step - 1, 1)
             if ended_3 is not None:
                 expand(ended_3)
             if ended_1 is not None:

@@ -30,15 +30,16 @@ BANK_GROUPS = 2
 ROUND_K = ROUND_GROUPS * K_PASS
 ROUNDS_PER_BATCH = GROUPS // ROUND_GROUPS
 ROUNDS = BATCH * ROUNDS_PER_BATCH
+SPREAD_STEP = 4
 ATTN_BUFS = 10
 
 FLOPS = 2 * BATCH * TOKENS * D_V * D + 2 * BATCH * TOKENS * D * D
 
 
-def batch_ending_at(round_index):
-    if 0 <= round_index < ROUNDS and round_index % ROUNDS_PER_BATCH == ROUNDS_PER_BATCH - 1:
-        return round_index // ROUNDS_PER_BATCH
-    return None
+ORDER = [(b, part) for part in range(ROUNDS_PER_BATCH) for b in (0, 1)] + [
+    (b, part) for b in (2, 3) for part in range(ROUNDS_PER_BATCH)
+]
+LAST_ROUND = [ORDER.index((b, ROUNDS_PER_BATCH - 1)) for b in range(BATCH)]
 
 
 def tile_attentionblock_pc_k_kernel(
@@ -52,29 +53,26 @@ def tile_attentionblock_pc_k_kernel(
         x_pool = ctx.enter_context(tc.tile_pool(name="x", bufs=BATCH))
         stage = ctx.enter_context(tc.tile_pool(name="stage", bufs=2))
         tail = ctx.enter_context(tc.tile_pool(name="tail", bufs=2))
-        acc_pool = ctx.enter_context(tc.psum_pool(name="acc", bufs=1))
-        work = ctx.enter_context(tc.psum_pool(name="work", bufs=6))
+        pairs = ctx.enter_context(tc.psum_pool(name="pairs", bufs=1))
+        work = ctx.enter_context(tc.psum_pool(name="work", bufs=4))
 
+        w_planes = [const.tile([P, D], U8, align_bytes=64, name="w_plane%d" % part) for part in range(ROUNDS_PER_BATCH)]
+        for plane in w_planes:
+            nc.vector.memset(plane[:].bitcast(I32), 0)
         bias_rows = const.tile([P, 2, D], BF16)
-        nc.vector.memset(bias_rows[:], 0.0)
-        nc.scalar.dma_start(out=bias_rows[0:1, 0, :], in_=b_merge.unsqueeze(0))
-        nc.scalar.dma_start(out=bias_rows[0:1, 1, :], in_=b1.unsqueeze(0))
+        nc.vector.memset(bias_rows[:].rearrange("p j f -> p (j f)").bitcast(I32), 0)
         gamma = const.tile([P, PACK], BF16)
         beta = const.tile([P, PACK], BF16)
-        nc.scalar.dma_start(out=gamma[:], in_=gamma2.rearrange("a b (p t) -> (a b p) t", t=PACK))
-        nc.scalar.dma_start(out=beta[:], in_=beta2.rearrange("a b (p t) -> (a b p) t", t=PACK))
         ones = const.tile([P, P], BF16)
         nc.vector.memset(ones[:], 1.0)
         eps = const.tile([P, 1], F32)
         nc.vector.memset(eps[:], EPS)
-        w_planes = const.tile([P, GROUPS, D], U8, align_bytes=64)
-        nc.vector.memset(w_planes[:].bitcast(I32), 0)
         w1_plane = const.tile([P, D], U8, align_bytes=64)
         nc.vector.memset(w1_plane[:].bitcast(I32), 0)
         ident = const.tile([P, P], F32)
         make_identity(nc, ident[:])
         table_warm = const.tile([P, 1], F32)
-        nc.scalar.activation(out=table_warm[:], in_=eps[:], func=ACT.Sqrt)
+        nc.scalar.activation(out=table_warm[:], in_=eps[:], func=ACT.Abs_reciprocal_sqrt)
 
         w_words = const.tile([P, GROUPS, D], U32, align_bytes=64)
         w1_words = const.tile([P, D], U32, align_bytes=64)
@@ -84,7 +82,7 @@ def tile_attentionblock_pc_k_kernel(
         x_of = {}
 
         def load_attn(r, by_token_tile):
-            b, part = divmod(r, ROUNDS_PER_BATCH)
+            b, part = ORDER[r]
             columns = slice(part * ROUND_K, (part + 1) * ROUND_K)
             attn_tile = attn_pool.tile([P, TILES, ROUND_K], BF16)
             if by_token_tile:
@@ -99,13 +97,12 @@ def tile_attentionblock_pc_k_kernel(
             nc.sync.dma_start(out=x_tile[:], in_=x[b].rearrange("(p i) f -> p i f", i=TILES))
             x_of[b] = x_tile
 
-        def load_scale_planes():
-            rows = W_merge_scales.rearrange("g q n -> q g n")
-            for low in range(2 * PACK):
-                quadrant, row = divmod(low, PACK)
+        def load_scale_planes(part):
+            groups = slice(part * ROUND_GROUPS, (part + 1) * ROUND_GROUPS)
+            for quadrant in range(4):
                 nc.sync.dma_start(
-                    out=w_planes[32 * quadrant + row : P : 64, :, :].bitcast(I32),
-                    in_=rows[low : 4 * PACK : 2 * PACK].bitcast(I32),
+                    out=w_planes[part][32 * quadrant : 32 * quadrant + 4 * ROUND_GROUPS, :].bitcast(I32),
+                    in_=W_merge_scales[groups, 4 * quadrant : 4 * quadrant + 4, :].bitcast(I32),
                 )
 
         def load_merge_weights(part):
@@ -123,17 +120,30 @@ def tile_attentionblock_pc_k_kernel(
                     in_=W1_scales[0, row : 4 * PACK : PACK, :].bitcast(I32),
                 )
 
+        def load_small_operands():
+            nc.sync.dma_start(out=bias_rows[0:1, 0, :], in_=b_merge.unsqueeze(0))
+            nc.sync.dma_start(out=bias_rows[0:1, 1, :], in_=b1.unsqueeze(0))
+            nc.sync.dma_start(out=gamma[:], in_=gamma2.rearrange("a b (p t) -> (a b p) t", t=PACK))
+            nc.sync.dma_start(out=beta[:], in_=beta2.rearrange("a b (p t) -> (a b p) t", t=PACK))
+
         def load_for_step(step):
             if step < ROUNDS:
                 load_attn(step, by_token_tile=(step == 0))
-            if step == 1:
-                load_scale_planes()
-            if 1 <= step <= ROUNDS_PER_BATCH:
-                load_merge_weights(step - 1)
-            if batch_ending_at(step - 1) is not None:
-                load_x(batch_ending_at(step - 1))
-            if step == ROUNDS_PER_BATCH:
+            part, turn = divmod(step, 2)
+            if part < ROUNDS_PER_BATCH:
+                if turn == 0:
+                    load_scale_planes(part)
+                else:
+                    load_merge_weights(part)
+            if step == SPREAD_STEP:
+                load_small_operands()
+            if step == 2 * ROUNDS_PER_BATCH:
+                load_x(0)
+                load_x(1)
                 load_expand_weights()
+            if step == 2 * ROUNDS_PER_BATCH + 1:
+                load_x(2)
+                load_x(3)
 
         for step in range(ATTN_BUFS):
             load_for_step(step)
@@ -184,9 +194,9 @@ def tile_attentionblock_pc_k_kernel(
             codes_of[r] = (codes, scales)
 
         def merge_passes(r, i):
-            b, part = divmod(r, ROUNDS_PER_BATCH)
+            b, part = ORDER[r]
             if part == 0:
-                acc_of[(b, i)] = acc_pool.tile([P, D], F32, name="acc%d" % i)
+                acc_of[(b, i)] = pairs.tile([P, D], F32, name="sums", tag="pair%d%d" % (b % 2, i))
             codes, scales = codes_of[r]
             for g in range(ROUND_GROUPS):
                 group = part * ROUND_GROUPS + g
@@ -196,7 +206,7 @@ def tile_attentionblock_pc_k_kernel(
                     lhsT=codes[:, i, cols].bitcast(FP8X4),
                     lhsT_scale=scales[:, i, cols],
                     rhs=w_words[:, group, :].bitcast(FP8X4),
-                    rhs_scale=w_planes[:, group, :],
+                    rhs_scale=w_planes[part][4 * g : P, :],
                     start=(group == 0),
                     stop=(group == GROUPS - 1),
                 )
@@ -204,7 +214,12 @@ def tile_attentionblock_pc_k_kernel(
         xb_of = {}
         x2_of = {}
         x2T_of = {}
+        stats_of = {}
+        rstd_of = {}
+        gain_of = {}
+        xnT_of = {}
         xn_of = {}
+        products_of = {}
 
         def prepare_residual(b):
             xb = tail.tile([P, TILES, D], F32)
@@ -213,56 +228,72 @@ def tile_attentionblock_pc_k_kernel(
             )
             xb_of[b] = xb
 
-        def residual(b):
-            x2 = tail.tile([P, TILES, D], F32)
-            for i in range(TILES):
-                nc.vector.tensor_tensor(out=x2[:, i, :], in0=acc_of[(b, i)][:], in1=xb_of[b][:, i, :], op=ALU.add)
-            nc.sync.dma_start(out=out_0[b].rearrange("(p i) f -> p i f", i=TILES), in_=x2[:])
-            x2_of[b] = x2
+        def residual(b, i):
+            if i == 0:
+                x2_of[b] = tail.tile([P, TILES, D], F32, name="x2")
+            x2 = x2_of[b]
+            nc.vector.tensor_tensor(out=x2[:, i, :], in0=acc_of[(b, i)][:], in1=xb_of[b][:, i, :], op=ALU.add)
+            if i == TILES - 1:
+                nc.sync.dma_start(out=out_0[b].rearrange("(p i) f -> p i f", i=TILES), in_=x2[:])
 
         def transpose_x2(b):
-            x2T_of[b] = [work.tile([P, 2, TOKENS], F32, tag="work", name="x2T%d" % h) for h in range(2)]
+            side = 1 if b < 2 else 0
+            x2T_of[b] = [pairs.tile([P, 2, TOKENS], F32, tag="pair%d%d" % (side, h), name="x2T%d" % h) for h in range(2)]
             for i in range(TILES):
                 for t in range(PACK):
                     nc.tensor.transpose(
                         x2T_of[b][t // 2][:, t % 2, i * P : (i + 1) * P], x2_of[b][:, i, t:D:PACK], ident[:]
                     )
 
-        def normalise(b):
-            columns = [x2T_of[b][t // 2][:, t % 2, :] for t in range(PACK)]
-            stats = tail.tile([P, PACK, 6], F32)
-            mean_var = tail.tile([P, PACK, 2], F32)
-            for t in range(PACK):
-                nc.vector.bn_stats(out=stats[:, t, :], in_=columns[t])
-            for t in range(PACK):
-                nc.vector.bn_aggr(out=mean_var[:, t, :], in_=stats[:, t, :])
-            std = tail.tile([P, PACK], F32)
-            nc.scalar.activation(out=std[:], in_=mean_var[:, :, 1], func=ACT.Sqrt, bias=eps[:, 0:1], scale=1.0)
-            gain = tail.tile([P, PACK], F32)
-            shift = tail.tile([P, PACK], F32)
-            nc.vector.reciprocal(out=gain[:], in_=std[:])
-            nc.vector.tensor_tensor(out=gain[:], in0=gain[:], in1=gamma[:], op=ALU.mult)
-            nc.vector.tensor_tensor(out=shift[:], in0=mean_var[:, :, 0], in1=gain[:], op=ALU.mult)
+        def statistics(b):
+            stats = tail.tile([P, 2, 2, 3], F32, name="stats")
+            for h in range(2):
+                nc.vector.bn_stats(
+                    out=stats[:, h].rearrange("p e s -> p (e s)"), in_=x2T_of[b][h][:].rearrange("p e k -> p k e")
+                )
+            stats_of[b] = stats[:].rearrange("p h e s -> p (h e) s")
+
+        def scale_of_norm(b):
+            rstd = tail.tile([P, PACK], F32, name="rstd")
+            nc.scalar.activation(
+                out=rstd[:], in_=stats_of[b][:, :, 2], func=ACT.Abs_reciprocal_sqrt, bias=eps[:, 0:1], scale=1.0 / TOKENS
+            )
+            rstd_of[b] = rstd
+
+        def gain_and_shift(b):
+            rstd = rstd_of[b]
+            gain = tail.tile([P, PACK], F32, name="gain")
+            shift = tail.tile([P, PACK], F32, name="shift")
+            nc.vector.tensor_tensor(out=gain[:], in0=rstd[:], in1=gamma[:], op=ALU.mult)
+            nc.vector.tensor_tensor(out=shift[:], in0=stats_of[b][:, :, 1], in1=gain[:], op=ALU.mult)
             nc.vector.tensor_tensor(out=shift[:], in0=beta[:], in1=shift[:], op=ALU.subtract)
-            xnT = tail.tile([P, PACK, TOKENS], BF16)
+            gain_of[b] = (gain, shift)
+
+        def normalise(b):
+            gain, shift = gain_of[b]
+            xnT = tail.tile([P, PACK, TOKENS], BF16, name="xnT")
             for t in range(PACK):
+                column = x2T_of[b][t // 2][:, t % 2, :]
                 if t < PACK // 2:
                     nc.scalar.activation(
-                        out=xnT[:, t, :], in_=columns[t], func=ACT.Identity, bias=shift[:, t : t + 1], scale=gain[:, t : t + 1]
+                        out=xnT[:, t, :], in_=column, func=ACT.Identity, bias=shift[:, t : t + 1], scale=gain[:, t : t + 1]
                     )
                 else:
                     nc.vector.tensor_scalar(
                         out=xnT[:, t, :],
-                        in0=columns[t],
+                        in0=column,
                         scalar1=gain[:, t : t + 1],
                         scalar2=shift[:, t : t + 1],
                         op0=ALU.mult,
                         op1=ALU.add,
                     )
-            xn_grouped = tail.tile([P, TOKENS, PACK], BF16, align_bytes=64)
-            nc.vector.tensor_copy(out=xn_grouped[:], in_=xnT[:].rearrange("p t k -> p k t"))
-            xn_codes = tail.tile([P, TOKENS], U32, align_bytes=64)
-            xn_scales = tail.tile([P, TOKENS], U8, align_bytes=64)
+            xnT_of[b] = xnT
+
+        def quantise_xn(b):
+            xn_grouped = tail.tile([P, TOKENS, PACK], BF16, align_bytes=64, name="xn_grouped")
+            nc.vector.tensor_copy(out=xn_grouped[:], in_=xnT_of[b][:].rearrange("p t k -> p k t"))
+            xn_codes = tail.tile([P, TOKENS], U32, align_bytes=64, name="xn_codes")
+            xn_scales = tail.tile([P, TOKENS], U8, align_bytes=64, name="xn_scales")
             nc.vector.quantize_mx(
                 out=xn_codes[:].bitcast(FP8X4), scales=xn_scales[:], in_=xn_grouped[:].rearrange("p k t -> p (k t)")
             )
@@ -282,43 +313,72 @@ def tile_attentionblock_pc_k_kernel(
                     start=True,
                     stop=True,
                 )
-            ffh = tail.tile([P, TILES, D], F32)
+            products_of[b] = products
+
+        def finish(b):
+            ffh = tail.tile([P, TILES, D], F32, name="ffh")
             ffh_rows = out_1[b].rearrange("(p i) f -> p i f", i=TILES)
             for i in range(TILES):
-                nc.vector.tensor_tensor(out=ffh[:, i, :], in0=products[i][:], in1=bias_all[:, 1, :], op=ALU.add)
+                nc.vector.tensor_tensor(out=ffh[:, i, :], in0=products_of[b][i][:], in1=bias_all[:, 1, :], op=ALU.add)
                 nc.sync.dma_start(out=ffh_rows[:, i, :], in_=ffh[:, i, :])
+
+        x2T_step = {}
+        for b in range(BATCH - 1):
+            x2T_step[b] = LAST_ROUND[max(b, 1)] + 2 if b != 1 else x2T_step[0] + 2
+        at_x2T = {s: b for b, s in x2T_step.items()}
+        at_stats = {s + 1: b for b, s in x2T_step.items()}
+        at_norm = {s + 2: b for b, s in x2T_step.items()}
+        at_end = {LAST_ROUND[b] + 1: b for b in range(BATCH)}
 
         open_sorted(0)
         sort_tile(0, 0, nc.vector.tensor_copy)
         sort_tile(0, 1, nc.scalar.copy)
         load_for_step(ATTN_BUFS)
-        for step in range(ROUNDS + 3):
-            ended_1 = batch_ending_at(step - 1)
-            ended_2 = batch_ending_at(step - 2)
-            ended_3 = batch_ending_at(step - 3)
-            if step < ROUNDS:
+        for step in range(ROUNDS + 1):
+            last = step == ROUNDS
+            if not last:
                 transpose_round(step)
-            if ended_1 is not None:
-                prepare_residual(ended_1)
             if step + 1 < ROUNDS:
                 open_sorted(step + 1)
                 sort_tile(step + 1, 0, nc.vector.tensor_copy)
-            if step < ROUNDS:
+            if step in at_stats:
+                statistics(at_stats[step])
+            if step in at_norm:
+                normalise(at_norm[step])
+                quantise_xn(at_norm[step])
+            if step in at_end:
+                prepare_residual(at_end[step])
+            if not last:
                 quantise_round(step)
             if step + 1 < ROUNDS:
                 sort_tile(step + 1, 1, nc.scalar.copy)
+            if step in at_stats:
+                scale_of_norm(at_stats[step])
+                gain_and_shift(at_stats[step])
             if step + 1 + ATTN_BUFS <= ROUNDS:
                 load_for_step(step + 1 + ATTN_BUFS)
-            if step == 0:
+            if step == SPREAD_STEP:
                 spread_biases()
-            if 1 <= step <= ROUNDS:
+            if step >= 1:
                 merge_passes(step - 1, 0)
-            if ended_2 is not None:
-                transpose_x2(ended_2)
-                normalise(ended_2)
-            if 1 <= step <= ROUNDS:
+            if step in at_x2T:
+                transpose_x2(at_x2T[step])
+            if step in at_norm:
+                expand(at_norm[step])
+            if step in at_end:
+                residual(at_end[step], 0)
+            if step >= 1:
                 merge_passes(step - 1, 1)
-            if ended_3 is not None:
-                expand(ended_3)
-            if ended_1 is not None:
-                residual(ended_1)
+            if step in at_end:
+                residual(at_end[step], 1)
+            if step in at_norm:
+                finish(at_norm[step])
+        b = BATCH - 1
+        transpose_x2(b)
+        statistics(b)
+        scale_of_norm(b)
+        gain_and_shift(b)
+        normalise(b)
+        quantise_xn(b)
+        expand(b)
+        finish(b)

@@ -30,7 +30,7 @@ BANK_GROUPS = 2
 ROUND_K = ROUND_GROUPS * K_PASS
 ROUNDS_PER_BATCH = GROUPS // ROUND_GROUPS
 ROUNDS = BATCH * ROUNDS_PER_BATCH
-SPREAD_STEP = 4
+V_ROUNDS = 8
 ATTN_BUFS = 10
 
 FLOPS = 2 * BATCH * TOKENS * D_V * D + 2 * BATCH * TOKENS * D * D
@@ -120,26 +120,30 @@ def tile_attentionblock_pc_k_kernel(
                     in_=W1_scales[0, row : 4 * PACK : PACK, :].bitcast(I32),
                 )
 
-        def load_small_operands():
+        def load_biases():
             nc.sync.dma_start(out=bias_rows[0:1, 0, :], in_=b_merge.unsqueeze(0))
             nc.sync.dma_start(out=bias_rows[0:1, 1, :], in_=b1.unsqueeze(0))
+
+        def load_gains():
             nc.sync.dma_start(out=gamma[:], in_=gamma2.rearrange("a b (p t) -> (a b p) t", t=PACK))
             nc.sync.dma_start(out=beta[:], in_=beta2.rearrange("a b (p t) -> (a b p) t", t=PACK))
 
         def load_for_step(step):
             if step < ROUNDS:
                 load_attn(step, by_token_tile=(step == 0))
+            if step == 1:
+                load_biases()
             part, turn = divmod(step, 2)
             if part < ROUNDS_PER_BATCH:
                 if turn == 0:
                     load_scale_planes(part)
                 else:
                     load_merge_weights(part)
-            if step == SPREAD_STEP:
-                load_small_operands()
-            if step == 2 * ROUNDS_PER_BATCH:
+            if step == 5:
                 load_x(0)
                 load_x(1)
+                load_gains()
+            if step == 2 * ROUNDS_PER_BATCH:
                 load_expand_weights()
             if step == 2 * ROUNDS_PER_BATCH + 1:
                 load_x(2)
@@ -152,7 +156,7 @@ def tile_attentionblock_pc_k_kernel(
 
         def spread_biases():
             for j in range(2):
-                spread = work.tile([P, D], F32, tag="work")
+                spread = pairs.tile([P, D], F32, tag="pair1%d" % j)
                 nc.tensor.matmul(out=spread[:], lhsT=ones[:], rhs=bias_rows[:, j, :], start=True, stop=True)
                 nc.vector.tensor_copy(out=bias_all[:, j, :], in_=spread[:])
 
@@ -160,6 +164,15 @@ def tile_attentionblock_pc_k_kernel(
         banks_of = {}
         codes_of = {}
         acc_of = {}
+
+        def sorter(r, i):
+            if i == 0:
+                return nc.vector
+            if r == 0:
+                return nc.scalar
+            if r < V_ROUNDS:
+                return nc.vector
+            return nc.scalar
 
         def open_sorted(r):
             sorted_of[r] = stage.tile([P, TILES, ROUND_GROUPS, HALVES, P], F32, name="sorted_words")
@@ -171,10 +184,15 @@ def tile_attentionblock_pc_k_kernel(
         def transpose_round(r):
             for i in range(TILES):
                 for first in range(0, ROUND_GROUPS, BANK_GROUPS):
-                    bank = work.tile([P, BANK_GROUPS, HALVES, P], F32, tag="work")
+                    bank = work.tile([P, HALVES, BANK_GROUPS, P], F32, tag="work")
                     for g in range(BANK_GROUPS):
                         for u in range(HALVES):
-                            nc.tensor.transpose(bank[:, g, u, :], sorted_of[r][:, i, first + g, u, :], ident[:])
+                            if sorter(r, i) is not None:
+                                words = sorted_of[r][:, i, first + g, u, :]
+                            else:
+                                begin = (first + g) * HALVES * P + u
+                                words = attn_of[r][:, i, :].bitcast(F32)[:, begin : begin + HALVES * P - 1 : HALVES]
+                            nc.tensor.transpose(bank[:, u, g, :], words, ident[:])
                     banks_of[(r, i, first)] = bank
 
         def quantise_round(r):
@@ -185,8 +203,12 @@ def tile_attentionblock_pc_k_kernel(
             for i in range(TILES):
                 for first in range(0, ROUND_GROUPS, BANK_GROUPS):
                     nc.scalar.copy(
-                        out=grouped_words[:, i, first : first + BANK_GROUPS, :].rearrange("p g (k u) -> p g k u", u=HALVES),
-                        in_=banks_of[(r, i, first)][:].rearrange("p g u k -> p g k u"),
+                        out=grouped_words[:, i, first : first + BANK_GROUPS, :]
+                        .rearrange("p g w -> p (g w)")
+                        .rearrange("p (c j u) -> p c u j", j=2, u=HALVES),
+                        in_=banks_of[(r, i, first)][:]
+                        .rearrange("p u g k -> p u (g k)")
+                        .rearrange("p u (c j) -> p c u j", j=2),
                     )
                 nc.vector.quantize_mx(
                     out=codes[:, i, :].bitcast(FP8X4), scales=scales[:, i, :], in_=grouped[:, i].rearrange("p g c -> p (g c)")
@@ -215,6 +237,7 @@ def tile_attentionblock_pc_k_kernel(
         x2_of = {}
         x2T_of = {}
         stats_of = {}
+        scaled_mean_of = {}
         rstd_of = {}
         gain_of = {}
         xnT_of = {}
@@ -252,6 +275,9 @@ def tile_attentionblock_pc_k_kernel(
                     out=stats[:, h].rearrange("p e s -> p (e s)"), in_=x2T_of[b][h][:].rearrange("p e k -> p k e")
                 )
             stats_of[b] = stats[:].rearrange("p h e s -> p (h e) s")
+            scaled_mean = tail.tile([P, PACK], F32, name="scaled_mean")
+            nc.vector.tensor_tensor(out=scaled_mean[:], in0=stats_of[b][:, :, 1], in1=gamma[:], op=ALU.mult)
+            scaled_mean_of[b] = scaled_mean
 
         def scale_of_norm(b):
             rstd = tail.tile([P, PACK], F32, name="rstd")
@@ -264,8 +290,8 @@ def tile_attentionblock_pc_k_kernel(
             rstd = rstd_of[b]
             gain = tail.tile([P, PACK], F32, name="gain")
             shift = tail.tile([P, PACK], F32, name="shift")
+            nc.vector.tensor_tensor(out=shift[:], in0=rstd[:], in1=scaled_mean_of[b][:], op=ALU.mult)
             nc.vector.tensor_tensor(out=gain[:], in0=rstd[:], in1=gamma[:], op=ALU.mult)
-            nc.vector.tensor_tensor(out=shift[:], in0=stats_of[b][:, :, 1], in1=gain[:], op=ALU.mult)
             nc.vector.tensor_tensor(out=shift[:], in0=beta[:], in1=shift[:], op=ALU.subtract)
             gain_of[b] = (gain, shift)
 
@@ -291,12 +317,20 @@ def tile_attentionblock_pc_k_kernel(
 
         def quantise_xn(b):
             xn_grouped = tail.tile([P, TOKENS, PACK], BF16, align_bytes=64, name="xn_grouped")
-            nc.vector.tensor_copy(out=xn_grouped[:], in_=xnT_of[b][:].rearrange("p t k -> p k t"))
             xn_codes = tail.tile([P, TOKENS], U32, align_bytes=64, name="xn_codes")
             xn_scales = tail.tile([P, TOKENS], U8, align_bytes=64, name="xn_scales")
-            nc.vector.quantize_mx(
-                out=xn_codes[:].bitcast(FP8X4), scales=xn_scales[:], in_=xn_grouped[:].rearrange("p k t -> p (k t)")
-            )
+            if b < BATCH - 1:
+                parts = [(slice(0, TOKENS), nc.vector.tensor_copy)]
+            else:
+                parts = [(slice(0, P), nc.vector.tensor_copy), (slice(P, TOKENS), nc.scalar.copy)]
+            for cols, copy in parts:
+                copy(out=xn_grouped[:, cols, :], in_=xnT_of[b][:, :, cols].rearrange("p t k -> p k t"))
+            for cols, copy in parts:
+                nc.vector.quantize_mx(
+                    out=xn_codes[:, cols].bitcast(FP8X4),
+                    scales=xn_scales[:, cols],
+                    in_=xn_grouped[:, cols, :].rearrange("p k t -> p (k t)"),
+                )
             xn_of[b] = (xn_codes, xn_scales)
 
         def expand(b):
@@ -328,51 +362,54 @@ def tile_attentionblock_pc_k_kernel(
         at_x2T = {s: b for b, s in x2T_step.items()}
         at_stats = {s + 1: b for b, s in x2T_step.items()}
         at_norm = {s + 2: b for b, s in x2T_step.items()}
+        at_ffh = {s + 3: b for b, s in x2T_step.items()}
         at_end = {LAST_ROUND[b] + 1: b for b in range(BATCH)}
+        at_xb = {6: 0, 7: 1, 8: 2, 9: 3}
 
         open_sorted(0)
         sort_tile(0, 0, nc.vector.tensor_copy)
         sort_tile(0, 1, nc.scalar.copy)
-        load_for_step(ATTN_BUFS)
         for step in range(ROUNDS + 1):
             last = step == ROUNDS
             if not last:
                 transpose_round(step)
             if step + 1 < ROUNDS:
                 open_sorted(step + 1)
-                sort_tile(step + 1, 0, nc.vector.tensor_copy)
+                for i in range(TILES):
+                    if sorter(step + 1, i) is nc.vector:
+                        sort_tile(step + 1, i, nc.vector.tensor_copy)
+                    elif sorter(step + 1, i) is nc.scalar:
+                        sort_tile(step + 1, i, nc.scalar.copy)
             if step in at_stats:
                 statistics(at_stats[step])
             if step in at_norm:
                 normalise(at_norm[step])
                 quantise_xn(at_norm[step])
-            if step in at_end:
-                prepare_residual(at_end[step])
+            if step in at_xb:
+                prepare_residual(at_xb[step])
             if not last:
                 quantise_round(step)
-            if step + 1 < ROUNDS:
-                sort_tile(step + 1, 1, nc.scalar.copy)
             if step in at_stats:
                 scale_of_norm(at_stats[step])
                 gain_and_shift(at_stats[step])
-            if step + 1 + ATTN_BUFS <= ROUNDS:
-                load_for_step(step + 1 + ATTN_BUFS)
-            if step == SPREAD_STEP:
-                spread_biases()
+            if step + ATTN_BUFS <= ROUNDS:
+                load_for_step(step + ATTN_BUFS)
             if step >= 1:
                 merge_passes(step - 1, 0)
             if step in at_x2T:
                 transpose_x2(at_x2T[step])
-            if step in at_norm:
-                expand(at_norm[step])
+            if step in at_ffh:
+                expand(at_ffh[step])
             if step in at_end:
                 residual(at_end[step], 0)
             if step >= 1:
                 merge_passes(step - 1, 1)
+            if step == 0:
+                spread_biases()
             if step in at_end:
                 residual(at_end[step], 1)
-            if step in at_norm:
-                finish(at_norm[step])
+            if step in at_ffh:
+                finish(at_ffh[step])
         b = BATCH - 1
         transpose_x2(b)
         statistics(b)

@@ -175,11 +175,14 @@ def tile_attentionblock_pc_k_kernel(
             return nc.scalar
 
         def open_sorted(r):
-            sorted_of[r] = stage.tile([P, TILES, ROUND_GROUPS, HALVES, P], F32, name="sorted_words")
+            sorted_of[r] = stage.tile([P, TILES, HALVES, ROUND_GROUPS * P], F32, name="sorted_words")
 
         def sort_tile(r, i, copy):
             words = attn_of[r][:].bitcast(F32)
-            copy(out=sorted_of[r][:, i], in_=words[:, i, :].rearrange("p (g j u) -> p g u j", g=ROUND_GROUPS, u=HALVES))
+            copy(
+                out=sorted_of[r][:, i].rearrange("p u (c j) -> p c u j", j=4),
+                in_=words[:, i, :].rearrange("p (c j u) -> p c u j", j=4, u=HALVES),
+            )
 
         def transpose_round(r):
             for i in range(TILES):
@@ -188,7 +191,7 @@ def tile_attentionblock_pc_k_kernel(
                     for g in range(BANK_GROUPS):
                         for u in range(HALVES):
                             if sorter(r, i) is not None:
-                                words = sorted_of[r][:, i, first + g, u, :]
+                                words = sorted_of[r][:, i, u, (first + g) * P : (first + g + 1) * P]
                             else:
                                 begin = (first + g) * HALVES * P + u
                                 words = attn_of[r][:, i, :].bitcast(F32)[:, begin : begin + HALVES * P - 1 : HALVES]

@@ -31,6 +31,7 @@ ROUND_K = ROUND_GROUPS * K_PASS
 ROUNDS_PER_BATCH = GROUPS // ROUND_GROUPS
 ROUNDS = BATCH * ROUNDS_PER_BATCH
 V_ROUNDS = 8
+WARM = (6, 0)
 ATTN_BUFS = 10
 
 FLOPS = 2 * BATCH * TOKENS * D_V * D + 2 * BATCH * TOKENS * D * D
@@ -56,6 +57,10 @@ def tile_attentionblock_pc_k_kernel(
         pairs = ctx.enter_context(tc.psum_pool(name="pairs", bufs=1))
         work = ctx.enter_context(tc.psum_pool(name="work", bufs=4))
 
+        ones = const.tile([P, P], BF16)
+        nc.vector.memset(ones[:], 1.0)
+        warm_rows = const.tile([P, D], BF16)
+        nc.vector.memset(warm_rows[:], 1.0)
         w_planes = [const.tile([P, D], U8, align_bytes=64, name="w_plane%d" % part) for part in range(ROUNDS_PER_BATCH)]
         for plane in w_planes:
             nc.vector.memset(plane[:].bitcast(I32), 0)
@@ -63,8 +68,6 @@ def tile_attentionblock_pc_k_kernel(
         nc.vector.memset(bias_rows[:].rearrange("p j f -> p (j f)").bitcast(I32), 0)
         gamma = const.tile([P, PACK], BF16)
         beta = const.tile([P, PACK], BF16)
-        ones = const.tile([P, P], BF16)
-        nc.vector.memset(ones[:], 1.0)
         eps = const.tile([P, 1], F32)
         nc.vector.memset(eps[:], EPS)
         w1_plane = const.tile([P, D], U8, align_bytes=64)
@@ -131,14 +134,12 @@ def tile_attentionblock_pc_k_kernel(
         def load_for_step(step):
             if step < ROUNDS:
                 load_attn(step, by_token_tile=(step == 0))
+            part, turn = divmod(step, 2)
+            if turn == 0 and part < ROUNDS_PER_BATCH:
+                load_scale_planes(part)
+                load_merge_weights(part)
             if step == 1:
                 load_biases()
-            part, turn = divmod(step, 2)
-            if part < ROUNDS_PER_BATCH:
-                if turn == 0:
-                    load_scale_planes(part)
-                else:
-                    load_merge_weights(part)
             if step == 5:
                 load_x(0)
                 load_x(1)
@@ -151,6 +152,11 @@ def tile_attentionblock_pc_k_kernel(
 
         for step in range(ATTN_BUFS):
             load_for_step(step)
+
+        def keep_warm(count):
+            bank = pairs.tile([P, D], F32, tag="pair10", name="warm")
+            for turn in range(count):
+                nc.tensor.matmul(out=bank[:], lhsT=ones[:], rhs=warm_rows[:], start=True, stop=True)
 
         bias_all = const.tile([P, 2, D], F32)
 
@@ -168,8 +174,6 @@ def tile_attentionblock_pc_k_kernel(
         def sorter(r, i):
             if i == 0:
                 return nc.vector
-            if r == 0:
-                return nc.scalar
             if r < V_ROUNDS:
                 return nc.vector
             return nc.scalar
@@ -365,17 +369,24 @@ def tile_attentionblock_pc_k_kernel(
         at_x2T = {s: b for b, s in x2T_step.items()}
         at_stats = {s + 1: b for b, s in x2T_step.items()}
         at_norm = {s + 2: b for b, s in x2T_step.items()}
-        at_ffh = {s + 3: b for b, s in x2T_step.items()}
+        at_ffh = {13: 0, 14: 1, 16: 2}
         at_end = {LAST_ROUND[b] + 1: b for b in range(BATCH)}
         at_xb = {6: 0, 7: 1, 8: 2, 9: 3}
 
+        keep_warm(WARM[0])
         open_sorted(0)
         sort_tile(0, 0, nc.vector.tensor_copy)
-        sort_tile(0, 1, nc.scalar.copy)
+        sort_tile(0, 1, nc.vector.tensor_copy)
         for step in range(ROUNDS + 1):
             last = step == ROUNDS
+            if step == 1:
+                merge_passes(0, 0)
+                merge_passes(0, 1)
             if not last:
                 transpose_round(step)
+            if step == 0:
+                keep_warm(WARM[1])
+                quantise_round(0)
             if step + 1 < ROUNDS:
                 open_sorted(step + 1)
                 for i in range(TILES):
@@ -390,14 +401,14 @@ def tile_attentionblock_pc_k_kernel(
                 quantise_xn(at_norm[step])
             if step in at_xb:
                 prepare_residual(at_xb[step])
-            if not last:
+            if 0 < step < ROUNDS:
                 quantise_round(step)
             if step in at_stats:
                 scale_of_norm(at_stats[step])
                 gain_and_shift(at_stats[step])
             if step + ATTN_BUFS <= ROUNDS:
                 load_for_step(step + ATTN_BUFS)
-            if step >= 1:
+            if step >= 2:
                 merge_passes(step - 1, 0)
             if step in at_x2T:
                 transpose_x2(at_x2T[step])
@@ -405,9 +416,9 @@ def tile_attentionblock_pc_k_kernel(
                 expand(at_ffh[step])
             if step in at_end:
                 residual(at_end[step], 0)
-            if step >= 1:
+            if step >= 2:
                 merge_passes(step - 1, 1)
-            if step == 0:
+            if step == 1:
                 spread_biases()
             if step in at_end:
                 residual(at_end[step], 1)

@@ -31,6 +31,7 @@ ROUND_K = ROUND_GROUPS * K_PASS
 ROUNDS_PER_BATCH = GROUPS // ROUND_GROUPS
 ROUNDS = BATCH * ROUNDS_PER_BATCH
 V_ROUNDS = 8
+TAILW = 8
 WARM = (6, 0)
 ATTN_BUFS = 10
 
@@ -158,13 +159,18 @@ def tile_attentionblock_pc_k_kernel(
             for turn in range(count):
                 nc.tensor.matmul(out=bank[:], lhsT=ones[:], rhs=warm_rows[:], start=True, stop=True)
 
+        spread_of = []
         bias_all = const.tile([P, 2, D], F32)
 
         def spread_biases():
             for j in range(2):
                 spread = pairs.tile([P, D], F32, tag="pair1%d" % j)
                 nc.tensor.matmul(out=spread[:], lhsT=ones[:], rhs=bias_rows[:, j, :], start=True, stop=True)
-                nc.vector.tensor_copy(out=bias_all[:, j, :], in_=spread[:])
+                spread_of.append(spread)
+
+        def keep_biases():
+            for j in range(2):
+                nc.vector.tensor_copy(out=bias_all[:, j, :], in_=spread_of[j][:])
 
         sorted_of = {}
         banks_of = {}
@@ -217,6 +223,8 @@ def tile_attentionblock_pc_k_kernel(
                         .rearrange("p u g k -> p u (g k)")
                         .rearrange("p u (c j) -> p c u j", j=2),
                     )
+                if r == 1 and i == 1:
+                    keep_biases()
                 nc.vector.quantize_mx(
                     out=codes[:, i, :].bitcast(FP8X4), scales=scales[:, i, :], in_=grouped[:, i].rearrange("p g c -> p (g c)")
                 )
@@ -360,8 +368,13 @@ def tile_attentionblock_pc_k_kernel(
             ffh = tail.tile([P, TILES, D], F32, name="ffh")
             ffh_rows = out_1[b].rearrange("(p i) f -> p i f", i=TILES)
             for i in range(TILES):
-                nc.vector.tensor_tensor(out=ffh[:, i, :], in0=products_of[b][i][:], in1=bias_all[:, 1, :], op=ALU.add)
-                nc.sync.dma_start(out=ffh_rows[:, i, :], in_=ffh[:, i, :])
+                pieces = 2 if b == BATCH - 1 else 1
+                for piece in range(pieces):
+                    cols = slice(piece * (D // pieces), (piece + 1) * (D // pieces))
+                    nc.vector.tensor_tensor(
+                        out=ffh[:, i, cols], in0=products_of[b][i][:, cols], in1=bias_all[:, 1, cols], op=ALU.add
+                    )
+                    nc.sync.dma_start(out=ffh_rows[:, i, cols], in_=ffh[:, i, cols])
 
         x2T_step = {}
         for b in range(BATCH - 1):
@@ -369,7 +382,7 @@ def tile_attentionblock_pc_k_kernel(
         at_x2T = {s: b for b, s in x2T_step.items()}
         at_stats = {s + 1: b for b, s in x2T_step.items()}
         at_norm = {s + 2: b for b, s in x2T_step.items()}
-        at_ffh = {13: 0, 14: 1, 16: 2}
+        at_ffh = {13: 0, 15: 1}
         at_end = {LAST_ROUND[b] + 1: b for b in range(BATCH)}
         at_xb = {6: 0, 7: 1, 8: 2, 9: 3}
 
@@ -379,11 +392,16 @@ def tile_attentionblock_pc_k_kernel(
         sort_tile(0, 1, nc.vector.tensor_copy)
         for step in range(ROUNDS + 1):
             last = step == ROUNDS
+            if last:
+                expand(2)
+                finish(2)
             if step == 1:
                 merge_passes(0, 0)
                 merge_passes(0, 1)
             if not last:
                 transpose_round(step)
+            if step == 1:
+                spread_biases()
             if step == 0:
                 keep_warm(WARM[1])
                 quantise_round(0)
@@ -418,14 +436,13 @@ def tile_attentionblock_pc_k_kernel(
                 residual(at_end[step], 0)
             if step >= 2:
                 merge_passes(step - 1, 1)
-            if step == 1:
-                spread_biases()
             if step in at_end:
                 residual(at_end[step], 1)
             if step in at_ffh:
                 finish(at_ffh[step])
         b = BATCH - 1
         transpose_x2(b)
+        keep_warm(TAILW)
         statistics(b)
         scale_of_norm(b)
         gain_and_shift(b)

from contextlib import ExitStack

import concourse.mybir as mybir
from concourse.masks import make_identity

FP8X4 = mybir.dt.float8_e4m3fn_x4
BF16 = mybir.dt.bfloat16
F32 = mybir.dt.float32
I32 = mybir.dt.int32
U32 = mybir.dt.uint32
U8 = mybir.dt.uint8
ALU = mybir.AluOpType
ACT = mybir.ActivationFunctionType

P = 128
PACK = 4
K_PASS = P * PACK
HALVES = 2

BATCH = 4
TOKENS = 256
TILES = TOKENS // P
D_V = 8192
D = 512
EPS = 1e-5

GROUPS = D_V // K_PASS
ROUND_GROUPS = 4
BANK_GROUPS = 2
ROUND_K = ROUND_GROUPS * K_PASS
ROUNDS_PER_BATCH = GROUPS // ROUND_GROUPS
ROUNDS = BATCH * ROUNDS_PER_BATCH
V_ROUNDS = 8
TAILW = 8
WARM = (6, 0)
ATTN_BUFS = 10

FLOPS = 2 * BATCH * TOKENS * D_V * D + 2 * BATCH * TOKENS * D * D


ORDER = [(b, part) for part in range(ROUNDS_PER_BATCH) for b in (0, 1)] + [
    (b, part) for b in (2, 3) for part in range(ROUNDS_PER_BATCH)
]
LAST_ROUND = [ORDER.index((b, ROUNDS_PER_BATCH - 1)) for b in range(BATCH)]


def tile_attentionblock_pc_k_kernel(
    tc, attn_out, x, W_merge_words, W_merge_scales, b_merge, gamma2, beta2, W1_words, W1_scales, b1, out_0, out_1
):
    nc = tc.nc
    with ExitStack() as ctx:
        ctx.enter_context(tc.manual_schedule())
        const = ctx.enter_context(tc.tile_pool(name="const", bufs=1))
        attn_pool = ctx.enter_context(tc.tile_pool(name="attn", bufs=ATTN_BUFS))
        x_pool = ctx.enter_context(tc.tile_pool(name="x", bufs=BATCH))
        stage = ctx.enter_context(tc.tile_pool(name="stage", bufs=2))
        tail = ctx.enter_context(tc.tile_pool(name="tail", bufs=2))
        pairs = ctx.enter_context(tc.psum_pool(name="pairs", bufs=1))
        work = ctx.enter_context(tc.psum_pool(name="work", bufs=4))

        ones = const.tile([P, P], BF16)
        nc.vector.memset(ones[:], 1.0)
        warm_rows = const.tile([P, D], BF16)
        nc.vector.memset(warm_rows[:], 1.0)
        w_planes = [const.tile([P, D], U8, align_bytes=64, name="w_plane%d" % part) for part in range(ROUNDS_PER_BATCH)]
        for plane in w_planes:
            nc.vector.memset(plane[:].bitcast(I32), 0)
        bias_rows = const.tile([P, 2, D], BF16)
        nc.vector.memset(bias_rows[:].rearrange("p j f -> p (j f)").bitcast(I32), 0)
        gamma = const.tile([P, PACK], BF16)
        beta = const.tile([P, PACK], BF16)
        eps = const.tile([P, 1], F32)
        nc.vector.memset(eps[:], EPS)
        w1_plane = const.tile([P, D], U8, align_bytes=64)
        nc.vector.memset(w1_plane[:].bitcast(I32), 0)
        ident = const.tile([P, P], F32)
        make_identity(nc, ident[:])
        table_warm = const.tile([P, 1], F32)
        nc.scalar.activation(out=table_warm[:], in_=eps[:], func=ACT.Abs_reciprocal_sqrt)

        w_words = const.tile([P, GROUPS, D], U32, align_bytes=64)
        w1_words = const.tile([P, D], U32, align_bytes=64)

        attn_rows = attn_out.rearrange("b (p i) k -> b p i k", i=TILES)
        attn_of = {}
        x_of = {}

        def load_attn(r, by_token_tile):
            b, part = ORDER[r]
            columns = slice(part * ROUND_K, (part + 1) * ROUND_K)
            attn_tile = attn_pool.tile([P, TILES, ROUND_K], BF16)
            if by_token_tile:
                for i in range(TILES):
                    nc.sync.dma_start(out=attn_tile[:, i, :], in_=attn_rows[b, :, i, columns])
            else:
                nc.sync.dma_start(out=attn_tile[:], in_=attn_rows[b, :, :, columns])
            attn_of[r] = attn_tile

        def load_x(b):
            x_tile = x_pool.tile([P, TILES, D], BF16)
            nc.sync.dma_start(out=x_tile[:], in_=x[b].rearrange("(p i) f -> p i f", i=TILES))
            x_of[b] = x_tile

        def load_scale_planes(part):
            groups = slice(part * ROUND_GROUPS, (part + 1) * ROUND_GROUPS)
            for quadrant in range(4):
                nc.sync.dma_start(
                    out=w_planes[part][32 * quadrant : 32 * quadrant + 4 * ROUND_GROUPS, :].bitcast(I32),
                    in_=W_merge_scales[groups, 4 * quadrant : 4 * quadrant + 4, :].bitcast(I32),
                )

        def load_merge_weights(part):
            groups = slice(part * ROUND_GROUPS, (part + 1) * ROUND_GROUPS)
            nc.sync.dma_start(
                out=w_words[:, groups, :].bitcast(I32),
                in_=W_merge_words[groups].rearrange("g p n t -> p g (n t)").bitcast(I32),
            )

        def load_expand_weights():
            nc.sync.dma_start(out=w1_words[:].bitcast(I32), in_=W1_words[0].rearrange("p n t -> p (n t)").bitcast(I32))
            for row in range(PACK):
                nc.sync.dma_start(
                    out=w1_plane[row:P:32, :].bitcast(I32),
                    in_=W1_scales[0, row : 4 * PACK : PACK, :].bitcast(I32),
                )

        def load_biases():
            nc.sync.dma_start(out=bias_rows[0:1, 0, :], in_=b_merge.unsqueeze(0))
            nc.sync.dma_start(out=bias_rows[0:1, 1, :], in_=b1.unsqueeze(0))

        def load_gains():
            nc.sync.dma_start(out=gamma[:], in_=gamma2.rearrange("a b (p t) -> (a b p) t", t=PACK))
            nc.sync.dma_start(out=beta[:], in_=beta2.rearrange("a b (p t) -> (a b p) t", t=PACK))

        def load_for_step(step):
            if step < ROUNDS:
                load_attn(step, by_token_tile=(step == 0))
            part, turn = divmod(step, 2)
            if turn == 0 and part < ROUNDS_PER_BATCH:
                load_scale_planes(part)
                load_merge_weights(part)
            if step == 1:
                load_biases()
            if step == 5:
                load_x(0)
                load_x(1)
                load_gains()
            if step == 2 * ROUNDS_PER_BATCH:
                load_expand_weights()
            if step == 2 * ROUNDS_PER_BATCH + 1:
                load_x(2)
                load_x(3)

        for step in range(ATTN_BUFS):
            load_for_step(step)

        def keep_warm(count):
            bank = pairs.tile([P, D], F32, tag="pair10", name="warm")
            for turn in range(count):
                nc.tensor.matmul(out=bank[:], lhsT=ones[:], rhs=warm_rows[:], start=True, stop=True)

        spread_of = []
        bias_all = const.tile([P, 2, D], F32)

        def spread_biases():
            for j in range(2):
                spread = pairs.tile([P, D], F32, tag="pair1%d" % j)
                nc.tensor.matmul(out=spread[:], lhsT=ones[:], rhs=bias_rows[:, j, :], start=True, stop=True)
                spread_of.append(spread)

        def keep_biases():
            for j in range(2):
                nc.vector.tensor_copy(out=bias_all[:, j, :], in_=spread_of[j][:])

        sorted_of = {}
        banks_of = {}
        codes_of = {}
        acc_of = {}

        def sorter(r, i):
            if i == 0:
                return nc.vector
            if r < V_ROUNDS:
                return nc.vector
            return nc.scalar

        def open_sorted(r):
            sorted_of[r] = stage.tile([P, TILES, HALVES, ROUND_GROUPS * P], F32, name="sorted_words")

        def sort_tile(r, i, copy):
            words = attn_of[r][:].bitcast(F32)
            copy(
                out=sorted_of[r][:, i].rearrange("p u (c j) -> p c u j", j=4),
                in_=words[:, i, :].rearrange("p (c j u) -> p c u j", j=4, u=HALVES),
            )

        def transpose_round(r):
            for i in range(TILES):
                for first in range(0, ROUND_GROUPS, BANK_GROUPS):
                    bank = work.tile([P, HALVES, BANK_GROUPS, P], F32, tag="work")
                    for g in range(BANK_GROUPS):
                        for u in range(HALVES):
                            if sorter(r, i) is not None:
                                words = sorted_of[r][:, i, u, (first + g) * P : (first + g + 1) * P]
                            else:
                                begin = (first + g) * HALVES * P + u
                                words = attn_of[r][:, i, :].bitcast(F32)[:, begin : begin + HALVES * P - 1 : HALVES]
                            nc.tensor.transpose(bank[:, u, g, :], words, ident[:])
                    banks_of[(r, i, first)] = bank

        def quantise_round(r):
            grouped = stage.tile([P, TILES, ROUND_GROUPS, P * PACK], BF16, align_bytes=64)
            grouped_words = grouped[:].bitcast(F32)
            codes = stage.tile([P, TILES, ROUND_GROUPS * P], U32, align_bytes=64)
            scales = stage.tile([P, TILES, ROUND_GROUPS * P], U8, align_bytes=64)
            for i in range(TILES):
                for first in range(0, ROUND_GROUPS, BANK_GROUPS):
                    nc.scalar.copy(
                        out=grouped_words[:, i, first : first + BANK_GROUPS, :]
                        .rearrange("p g w -> p (g w)")
                        .rearrange("p (c j u) -> p c u j", j=2, u=HALVES),
                        in_=banks_of[(r, i, first)][:]
                        .rearrange("p u g k -> p u (g k)")
                        .rearrange("p u (c j) -> p c u j", j=2),
                    )
                if r == 1 and i == 1:
                    keep_biases()
                nc.vector.quantize_mx(
                    out=codes[:, i, :].bitcast(FP8X4), scales=scales[:, i, :], in_=grouped[:, i].rearrange("p g c -> p (g c)")
                )
            codes_of[r] = (codes, scales)

        def merge_passes(r, i):
            b, part = ORDER[r]
            if part == 0:
                acc_of[(b, i)] = pairs.tile([P, D], F32, name="sums", tag="pair%d%d" % (b % 2, i))
            codes, scales = codes_of[r]
            for g in range(ROUND_GROUPS):
                group = part * ROUND_GROUPS + g
                cols = slice(g * P, (g + 1) * P)
                nc.tensor.matmul_mx(
                    out=acc_of[(b, i)][:],
                    lhsT=codes[:, i, cols].bitcast(FP8X4),
                    lhsT_scale=scales[:, i, cols],
                    rhs=w_words[:, group, :].bitcast(FP8X4),
                    rhs_scale=w_planes[part][4 * g : P, :],
                    start=(group == 0),
                    stop=(group == GROUPS - 1),
                )

        xb_of = {}
        x2_of = {}
        x2T_of = {}
        stats_of = {}
        scaled_mean_of = {}
        rstd_of = {}
        gain_of = {}
        xnT_of = {}
        xn_of = {}
        products_of = {}

        def prepare_residual(b):
            xb = tail.tile([P, TILES, D], F32)
            nc.vector.tensor_tensor(
                out=xb[:], in0=x_of[b][:], in1=bias_all[:, 0, :].unsqueeze(1).to_broadcast([P, TILES, D]), op=ALU.add
            )
            xb_of[b] = xb

        def residual(b, i):
            if i == 0:
                x2_of[b] = tail.tile([P, TILES, D], F32, name="x2")
            x2 = x2_of[b]
            nc.vector.tensor_tensor(out=x2[:, i, :], in0=acc_of[(b, i)][:], in1=xb_of[b][:, i, :], op=ALU.add)
            if i == TILES - 1:
                nc.sync.dma_start(out=out_0[b].rearrange("(p i) f -> p i f", i=TILES), in_=x2[:])

        def transpose_x2(b):
            side = 1 if b < 2 else 0
            x2T_of[b] = [pairs.tile([P, 2, TOKENS], F32, tag="pair%d%d" % (side, h), name="x2T%d" % h) for h in range(2)]
            for i in range(TILES):
                for t in range(PACK):
                    nc.tensor.transpose(
                        x2T_of[b][t // 2][:, t % 2, i * P : (i + 1) * P], x2_of[b][:, i, t:D:PACK], ident[:]
                    )

        def statistics(b):
            stats = tail.tile([P, 2, 2, 3], F32, name="stats")
            for h in range(2):
                nc.vector.bn_stats(
                    out=stats[:, h].rearrange("p e s -> p (e s)"), in_=x2T_of[b][h][:].rearrange("p e k -> p k e")
                )
            stats_of[b] = stats[:].rearrange("p h e s -> p (h e) s")
            scaled_mean = tail.tile([P, PACK], F32, name="scaled_mean")
            nc.vector.tensor_tensor(out=scaled_mean[:], in0=stats_of[b][:, :, 1], in1=gamma[:], op=ALU.mult)
            scaled_mean_of[b] = scaled_mean

        def scale_of_norm(b):
            rstd = tail.tile([P, PACK], F32, name="rstd")
            nc.scalar.activation(
                out=rstd[:], in_=stats_of[b][:, :, 2], func=ACT.Abs_reciprocal_sqrt, bias=eps[:, 0:1], scale=1.0 / TOKENS
            )
            rstd_of[b] = rstd

        def gain_and_shift(b):
            rstd = rstd_of[b]
            gain = tail.tile([P, PACK], F32, name="gain")
            shift = tail.tile([P, PACK], F32, name="shift")
            nc.vector.tensor_tensor(out=shift[:], in0=rstd[:], in1=scaled_mean_of[b][:], op=ALU.mult)
            nc.vector.tensor_tensor(out=gain[:], in0=rstd[:], in1=gamma[:], op=ALU.mult)
            nc.vector.tensor_tensor(out=shift[:], in0=beta[:], in1=shift[:], op=ALU.subtract)
            gain_of[b] = (gain, shift)

        def normalise(b):
            gain, shift = gain_of[b]
            xnT = tail.tile([P, PACK, TOKENS], BF16, name="xnT")
            for t in range(PACK):
                column = x2T_of[b][t // 2][:, t % 2, :]
                if t < PACK // 2:
                    nc.scalar.activation(
                        out=xnT[:, t, :], in_=column, func=ACT.Identity, bias=shift[:, t : t + 1], scale=gain[:, t : t + 1]
                    )
                else:
                    nc.vector.tensor_scalar(
                        out=xnT[:, t, :],
                        in0=column,
                        scalar1=gain[:, t : t + 1],
                        scalar2=shift[:, t : t + 1],
                        op0=ALU.mult,
                        op1=ALU.add,
                    )
            xnT_of[b] = xnT

        def quantise_xn(b):
            xn_grouped = tail.tile([P, TOKENS, PACK], BF16, align_bytes=64, name="xn_grouped")
            xn_codes = tail.tile([P, TOKENS], U32, align_bytes=64, name="xn_codes")
            xn_scales = tail.tile([P, TOKENS], U8, align_bytes=64, name="xn_scales")
            if b < BATCH - 1:
                parts = [(slice(0, TOKENS), nc.vector.tensor_copy)]
            else:
                parts = [(slice(0, P), nc.vector.tensor_copy), (slice(P, TOKENS), nc.scalar.copy)]
            for cols, copy in parts:
                copy(out=xn_grouped[:, cols, :], in_=xnT_of[b][:, :, cols].rearrange("p t k -> p k t"))
            for cols, copy in parts:
                nc.vector.quantize_mx(
                    out=xn_codes[:, cols].bitcast(FP8X4),
                    scales=xn_scales[:, cols],
                    in_=xn_grouped[:, cols, :].rearrange("p k t -> p (k t)"),
                )
            xn_of[b] = (xn_codes, xn_scales)

        def expand(b):
            xn_codes, xn_scales = xn_of[b]
            products = [work.tile([P, D], F32, tag="work", name="ffh_ps%d" % i) for i in range(TILES)]
            for i in range(TILES):
                cols = slice(i * P, (i + 1) * P)
                nc.tensor.matmul_mx(
                    out=products[i][:],
                    lhsT=xn_codes[:, cols].bitcast(FP8X4),
                    lhsT_scale=xn_scales[:, cols],
                    rhs=w1_words[:].bitcast(FP8X4),
                    rhs_scale=w1_plane[:],
                    start=True,
                    stop=True,
                )
            products_of[b] = products

        def finish(b):
            ffh = tail.tile([P, TILES, D], F32, name="ffh")
            ffh_rows = out_1[b].rearrange("(p i) f -> p i f", i=TILES)
            for i in range(TILES):
                pieces = 2 if b == BATCH - 1 else 1
                for piece in range(pieces):
                    cols = slice(piece * (D // pieces), (piece + 1) * (D // pieces))
                    nc.vector.tensor_tensor(
                        out=ffh[:, i, cols], in0=products_of[b][i][:, cols], in1=bias_all[:, 1, cols], op=ALU.add
                    )
                    nc.sync.dma_start(out=ffh_rows[:, i, cols], in_=ffh[:, i, cols])

        x2T_step = {}
        for b in range(BATCH - 1):
            x2T_step[b] = LAST_ROUND[max(b, 1)] + 2 if b != 1 else x2T_step[0] + 2
        at_x2T = {s: b for b, s in x2T_step.items()}
        at_stats = {s + 1: b for b, s in x2T_step.items()}
        at_norm = {s + 2: b for b, s in x2T_step.items()}
        at_ffh = {13: 0, 15: 1}
        at_end = {LAST_ROUND[b] + 1: b for b in range(BATCH)}
        at_xb = {6: 0, 7: 1, 8: 2, 9: 3}

        keep_warm(WARM[0])
        open_sorted(0)
        sort_tile(0, 0, nc.vector.tensor_copy)
        sort_tile(0, 1, nc.vector.tensor_copy)
        for step in range(ROUNDS + 1):
            last = step == ROUNDS
            if last:
                expand(2)
                finish(2)
            if step == 1:
                merge_passes(0, 0)
                merge_passes(0, 1)
            if not last:
                transpose_round(step)
            if step == 1:
                spread_biases()
            if step == 0:
                keep_warm(WARM[1])
                quantise_round(0)
            if step + 1 < ROUNDS:
                open_sorted(step + 1)
                for i in range(TILES):
                    if sorter(step + 1, i) is nc.vector:
                        sort_tile(step + 1, i, nc.vector.tensor_copy)
                    elif sorter(step + 1, i) is nc.scalar:
                        sort_tile(step + 1, i, nc.scalar.copy)
            if step in at_stats:
                statistics(at_stats[step])
            if step in at_norm:
                normalise(at_norm[step])
                quantise_xn(at_norm[step])
            if step in at_xb:
                prepare_residual(at_xb[step])
            if 0 < step < ROUNDS:
                quantise_round(step)
            if step in at_stats:
                scale_of_norm(at_stats[step])
                gain_and_shift(at_stats[step])
            if step + ATTN_BUFS <= ROUNDS:
                load_for_step(step + ATTN_BUFS)
            if step >= 2:
                merge_passes(step - 1, 0)
            if step in at_x2T:
                transpose_x2(at_x2T[step])
            if step in at_ffh:
                expand(at_ffh[step])
            if step in at_end:
                residual(at_end[step], 0)
            if step >= 2:
                merge_passes(step - 1, 1)
            if step in at_end:
                residual(at_end[step], 1)
            if step in at_ffh:
                finish(at_ffh[step])
        b = BATCH - 1
        transpose_x2(b)
        keep_warm(TAILW)
        statistics(b)
        scale_of_norm(b)
        gain_and_shift(b)
        normalise(b)
        quantise_xn(b)
        expand(b)
        finish(b)
